import numpy as np
import ml_dtypes


def mxq(x, axis, fmt="e4m3"):
    dtype, down = {"e4m3": (ml_dtypes.float8_e4m3fn, 7), "e5m2": (ml_dtypes.float8_e5m2, 14)}[fmt]
    v = np.moveaxis(np.asarray(x, np.float32).astype(ml_dtypes.bfloat16).astype(np.float64), axis, -1)
    blocks = v.reshape(v.shape[:-1] + (-1, 32))
    amax = np.abs(blocks).max(-1, keepdims=True)
    byte = np.maximum(np.where(amax > 0, np.frexp(amax)[1] - 1 + 127, 0) - down, 1)
    scale = np.exp2(byte - 127.0)
    codes = (blocks / scale).astype(np.float32).astype(dtype).astype(np.float64)
    return np.moveaxis((codes * scale).reshape(v.shape), -1, axis)


WIDE = False


def mx_kscale(k):
    if not WIDE:
        return np.ones(k)
    levels = np.array([10, -10, 5, -5, 0])
    if k % 512:
        return np.exp2(np.random.permutation(np.resize(levels, k // 32))).repeat(32)
    a = np.empty((k // 512, 16))
    for p in range(k // 512):
        a[p, :8] = np.random.permutation(np.resize(levels, 8))
        for g in range(8):
            far = levels[np.abs(levels - a[p, g]) >= 10]
            a[p, g + 8] = far[np.random.randint(len(far))]
    return np.exp2(a.ravel()).repeat(32)


BF16 = ml_dtypes.bfloat16


def bf(x):
    return np.asarray(x, np.float32).astype(BF16)


def f64(x):
    return np.asarray(x).astype(np.float64)


B, C, T, TF, CCONF, GROUPS = 48, 512, 64, 256, 512, 32
EPS = 1e-5
C2 = 2 * C


def group_norm(x, gamma, beta):
    b_, c_, t_ = x.shape
    xg = x.reshape(b_, GROUPS, c_ // GROUPS, t_)
    mu = xg.mean(axis=(2, 3), keepdims=True)
    var = xg.var(axis=(2, 3), keepdims=True)
    xg = (xg - mu) / np.sqrt(var + EPS)
    return xg.reshape(b_, c_, t_) * gamma[None, :, None] + beta[None, :, None]


def pool(fh, lo, hi):
    idx = np.arange(fh.shape[-1])
    out = np.empty((fh.shape[0], fh.shape[1], lo.shape[1]))
    for i in range(fh.shape[0]):
        mask = (idx[None, :] > lo[i][:, None] - 1.0) & (idx[None, :] <= hi[i][:, None])
        out[i] = np.where(mask[None, :, :], fh[i][:, None, :], -np.inf).max(-1)
    return np.where(np.isfinite(out), out, 0.0)


def boundary_max_pooling(feature, segments):
    tin = feature.shape[-1]
    half = feature.shape[1] // 2
    s = np.clip(segments, 0.0, tin - 1.0)
    left = pool(feature[:, :half], s[..., 0], s[..., 1])
    right = pool(feature[:, half:], s[..., 2], s[..., 3])
    return np.concatenate([left, right], axis=1)


def make_segments(n, tin):
    lo = np.random.uniform(size=(B, n, 2)) * (1.25 * tin) - 0.125 * tin
    ln = np.random.uniform(size=(B, n, 2)) * (tin / 4) + 1.0
    ln = np.where(np.random.uniform(size=(B, n, 2)) < 0.1, -ln, ln)
    hi = lo + ln
    return np.stack([lo[..., 0], hi[..., 0], lo[..., 1], hi[..., 1]], axis=-1)


def draw0():
    s = mx_kscale(C)
    return {
        'feature': bf(np.random.standard_normal((B, C, T)) * s[None, :, None]),
        'segments': bf(make_segments(T, T)),
        'w_lr': bf(np.random.standard_normal((C2, C)) * C ** -0.5 / s[None, :]),
        'b_lr': bf(np.random.standard_normal(C2) * 0.3),
        'g_lr': bf(1.0 + 0.2 * np.random.standard_normal(C2)),
        'be_lr': bf(np.random.standard_normal(C2) * 0.3),
    }


def core(feature, segments, w_lr, b_lr, g_lr, be_lr):
    y = (mxq(f64(w_lr), 1, 'e4m3') @ mxq(f64(feature), 1, 'e4m3')) + f64(b_lr)[None, :, None]
    feat2 = np.maximum(group_norm(y, f64(g_lr), f64(be_lr)), 0.0)
    return feat2, boundary_max_pooling(feat2, f64(segments))


def e4m3fn_bytes(y):
    return np.clip(np.asarray(y, np.float64), -448.0, 448.0).astype(np.float32).astype(ml_dtypes.float8_e4m3fn).view(np.uint8)


def e4m3fn_values(b):
    return np.asarray(b, np.uint8).view(ml_dtypes.float8_e4m3fn).astype(np.float64)


def setup_inputs():
    d = draw0()
    x0 = np.asarray(d['feature']).astype(np.float64)
    s = (np.max(np.abs(x0), axis=(0, 2), keepdims=True) / 448.0).astype(np.float32)
    out = {}
    for k, v in d.items():
        if k == 'feature':
            out['feature_bytes'] = e4m3fn_bytes(x0 / s.astype(np.float64))
            out['feature_scale'] = s
        else:
            out[k] = v
    return out


def reference(feature_bytes, feature_scale, segments, w_lr, b_lr, g_lr, be_lr):
    return core(e4m3fn_values(feature_bytes) * feature_scale.astype(np.float64), segments, w_lr, b_lr, g_lr, be_lr)

@@ -1,0 +1,407 @@
+from contextlib import ExitStack
+
+import concourse.bass as bass
+import concourse.mybir as mybir
+from concourse.masks import make_block_diagonal, make_identity
+
+F32 = mybir.dt.float32
+BF16 = mybir.dt.bfloat16
+I32 = mybir.dt.int32
+U32 = mybir.dt.uint32
+U8 = mybir.dt.uint8
+FP8 = mybir.dt.float8_e4m3fn
+FP8X4 = mybir.dt.float8_e4m3fn_x4
+ALU = mybir.AluOpType
+ACT = mybir.ActivationFunctionType
+AX = mybir.AxisListType
+
+FLOPS = 2 * 48 * 1024 * 512 * 64
+
+P = 128
+NB = 48
+NPAIR = 24
+ROT = 6
+NHOLD = 6
+PARK_ROWS = 1536
+EPS = 1e-5
+LAG = 2
+NTB = 2
+STAT_GROUPS = ((0, 2), (2, 6), (6, 12), (12, 18), (18, 24))
+
+
+def tile_coarsepyramid_pa_kernel(
+    tc, feature_bytes, feature_scale, segments, w_lr, b_lr, g_lr, be_lr, out_0, out_1
+):
+    nc = tc.nc
+    with ExitStack() as ctx:
+        const = ctx.enter_context(tc.tile_pool(name="const", bufs=1))
+        small = ctx.enter_context(tc.tile_pool(name="small", bufs=2))
+        ps_y = ctx.enter_context(tc.psum_pool(name="ps_y", bufs=3))
+        ps_tp = ctx.enter_context(tc.psum_pool(name="ps_tp", bufs=3))
+        ps_bk = ctx.enter_context(tc.psum_pool(name="ps_bk", bufs=1))
+        ps_st = ctx.enter_context(tc.psum_pool(name="ps_st", bufs=1))
+
+        ident = const.tile([P, P], F32)
+        make_identity(nc, ident[:])
+        ones8 = const.tile([P, P], F32)
+        make_block_diagonal(nc, ones8[:], 8)
+
+        xcodes = const.tile([P, NB * 64], U32, align_bytes=64)
+        xscales = const.tile([P, NB * 64], U8, align_bytes=64)
+        wcodes = const.tile([P, 1024], U32, align_bytes=64)
+        wscales = const.tile([P, 1024], U8, align_bytes=64)
+        stats = const.tile([P, 8, 2 * NB, 3], F32)
+        gain = const.tile([P, 8, NB], F32)
+        shift = const.tile([P, 8, NB], F32)
+        idx = const.tile([P, 2, 48], I32)
+        pv = const.tile([P, 3, 8], F32)
+        sc = const.tile([P, 4], F32)
+
+        with tc.tile_pool(name="prep", bufs=1) as prep, tc.tile_pool(name="prep2", bufs=2) as prep2:
+            xb = prep.tile([P, NB, 256], U8)
+            fv = feature_bytes.rearrange("b (p j) t -> p b (j t)", j=4)
+            nc.sync.dma_start(out=sc[:], in_=feature_scale.rearrange("o (p j) i -> p (o j i)", j=4))
+            w_sb = prep.tile([P, 2, 4, 512], BF16)
+
+            def load_bytes(p0, p1):
+                b0 = (p0 + 2 * ROT) % NB
+                nc.sync.dma_start(out=xb[:, p0:p1, :], in_=fv[:, b0:b0 + (p1 - p0), :])
+
+            load_bytes(0, 4)
+            nc.sync.dma_start(
+                out=w_sb[:].rearrange("q s u k -> q s (u k)"),
+                in_=w_lr.rearrange("(s q u) k -> q s (u k)", s=2, u=4),
+            )
+            for p0, p1 in ((4, 8), (8, 16), (16, 32), (32, 36), (36, 48)):
+                load_bytes(p0, p1)
+
+            pv_bf = prep.tile([P, 3, 16], BF16)
+            for m, vec in enumerate((b_lr, g_lr, be_lr)):
+                nc.scalar.dma_start(
+                    out=pv_bf[:, m, 0:8].rearrange("q (s u) -> q s u", s=2),
+                    in_=vec.rearrange("(s q u) -> q s u", s=2, u=4),
+                )
+            sg_bf = prep.tile([P, NPAIR, 4], BF16)
+            seg_v = segments.rearrange("(i c) n f -> c n i f", c=2)
+            for c in range(2):
+                nc.scalar.dma_start(out=sg_bf[c * 64:(c + 1) * 64, :, :], in_=seg_v[c])
+            nc.vector.tensor_copy(out=pv[:], in_=pv_bf[:, :, 0:8])
+
+            wg = prep.tile([P, 8, 128, 4], BF16, align_bytes=64)
+            for h in range(4):
+                xt = ps_tp.tile([P, 2, 2, 128], F32, tag="tp")
+                for a in range(2):
+                    tau = 2 * h + a
+                    words = w_sb[:, tau // 4, tau % 4, :].bitcast(F32)
+                    for v in range(2):
+                        nc.tensor.transpose(xt[:, a, v, :], words[:, v:256:2], ident[:])
+                nc.vector.tensor_copy(
+                    out=wg[:, 2 * h:2 * h + 2, :, :].rearrange("p a q e -> p a (q e)").bitcast(F32)
+                    .rearrange("p a (q v) -> p a q v", v=2),
+                    in_=xt[:].rearrange("p a v q -> p a q v"),
+                )
+            nc.vector.quantize_mx(
+                out=wcodes[:].bitcast(FP8X4), scales=wscales[:], in_=wg[:].rearrange("p a q e -> p (a q e)")
+            )
+
+            for ci, (p0, p1) in enumerate(((0, 4), (4, 8), (8, 16), (16, 32), (32, 48))):
+                n = p1 - p0
+                xc = prep2.tile([P, n * 256], BF16, tag="xc")
+                nc.scalar.copy(out=xc[:], in_=xb[:, p0:p1, :].rearrange("p b e -> p (b e)").bitcast(FP8))
+                gx = prep2.tile([P, n * 64, 4], BF16, tag="gx", align_bytes=64)
+                xc4 = xc[:].rearrange("p (b j t) -> p b j t", j=4, t=64)
+                gx4 = gx[:].rearrange("p (b t) j -> p b t j", t=64)
+                for j in range(4):
+                    if ci < 2:
+                        nc.vector.tensor_scalar(
+                            out=gx4[:, :, :, j], in0=xc4[:, :, j, :], scalar1=sc[:, j:j + 1], scalar2=None,
+                            op0=ALU.mult,
+                        )
+                    else:
+                        nc.gpsimd.tensor_scalar(
+                            out=gx4[:, :, :, j], in0=xc4[:, :, j, :], scalar1=sc[:, j:j + 1], scalar2=0.0,
+                            op0=ALU.mult, op1=ALU.add,
+                        )
+                nc.vector.quantize_mx(
+                    out=xcodes[:, p0 * 64:p1 * 64].bitcast(FP8X4),
+                    scales=xscales[:, p0 * 64:p1 * 64],
+                    in_=gx[:].rearrange("p c j -> p (c j)"),
+                )
+
+            xs = prep.tile([P, 96], F32)
+            nc.vector.tensor_scalar(
+                out=xs[:], in0=sg_bf[:].rearrange("p i f -> p (i f)"), scalar1=0.0, scalar2=63.0,
+                op0=ALU.max, op1=ALU.min,
+            )
+            xi = prep.tile([P, 96], I32)
+            nc.vector.tensor_copy(out=xi[:], in_=xs[:])
+            xf = prep.tile([P, 96], F32)
+            nc.vector.tensor_copy(out=xf[:], in_=xi[:])
+            gt = prep.tile([P, 96], F32)
+            nc.vector.tensor_tensor(out=gt[:], in0=xf[:], in1=xs[:], op=ALU.is_gt)
+            fl = prep.tile([P, 48, 2], F32)
+            nc.vector.tensor_tensor(out=fl[:].rearrange("p c e -> p (c e)"), in0=xf[:], in1=gt[:], op=ALU.subtract)
+            lo = fl[:, :, 0]
+            hi = fl[:, :, 1]
+            lm = prep.tile([P, 48], F32)
+            nc.vector.tensor_tensor(out=lm[:], in0=hi, in1=lo, op=ALU.subtract)
+            fk = prep.tile([P, 48, 5], F32)
+            fw = prep.tile([P, 48, 5], F32)
+            for j in range(1, 6):
+                thr = float(2 ** j - 1)
+                nc.vector.tensor_scalar(
+                    out=fk[:, :, j - 1], in0=lm[:], scalar1=thr, scalar2=2.0, op0=ALU.is_ge, op1=ALU.mult
+                )
+                nc.vector.tensor_scalar(
+                    out=fw[:, :, j - 1], in0=lm[:], scalar1=thr, scalar2=float(2 - 6 * 2 ** j),
+                    op0=ALU.is_ge, op1=ALU.mult,
+                )
+            k2 = prep.tile([P, 48], F32)
+            nc.vector.tensor_reduce(out=k2[:], in_=fk[:], axis=AX.X, op=ALU.add)
+            ue = prep.tile([P, 48], F32)
+            nc.vector.tensor_reduce(out=ue[:], in_=fw[:], axis=AX.X, op=ALU.add)
+            b12i = prep.tile([P, 48], I32)
+            for c in range(2):
+                nc.gpsimd.iota(
+                    b12i[c * 64:(c + 1) * 64, :], pattern=[[0, 24], [1, 2]], base=768 * c, channel_multiplier=0
+                )
+            b12 = prep.tile([P, 48], F32)
+            nc.vector.tensor_copy(out=b12[:], in_=b12i[:])
+            pidx = prep.tile([P, 1], I32)
+            nc.gpsimd.iota(pidx[:], pattern=[[0, 1]], base=0, channel_multiplier=1)
+            pand = prep.tile([P, 1], I32)
+            nc.vector.tensor_single_scalar(out=pand[:], in_=pidx[:], scalar=15, op=ALU.bitwise_and)
+            pf = prep.tile([P, 1], F32)
+            nc.vector.tensor_copy(out=pf[:], in_=pand[:])
+            zc = prep.tile([P, 1], F32)
+            nc.vector.tensor_scalar(out=zc[:], in0=pf[:], scalar1=12.0, scalar2=586.0, op0=ALU.mult, op1=ALU.add)
+            zidx = prep.tile([P, 48], F32)
+            nc.vector.tensor_scalar(out=zidx[:], in0=b12[:], scalar1=zc[:, 0:1], scalar2=None, op0=ALU.add)
+            for e, (pos, extra, thr) in enumerate(((lo, k2, 0.0), (hi, ue, 1.0))):
+                ri = prep.tile([P, 48], F32, name="ri%d" % e)
+                nc.vector.scalar_tensor_tensor(out=ri[:], in0=pos, scalar=12.0, in1=b12[:], op0=ALU.mult, op1=ALU.add)
+                nc.vector.tensor_tensor(out=ri[:], in0=ri[:], in1=extra[:], op=ALU.add)
+                nc.vector.tensor_tensor(out=ri[:], in0=ri[:], in1=zidx[:], op=ALU.subtract)
+                ne = prep.tile([P, 48], F32, name="ne%d" % e)
+                nc.vector.tensor_single_scalar(out=ne[:], in_=lm[:], scalar=thr, op=ALU.is_ge)
+                nc.vector.tensor_tensor(out=ri[:], in0=ri[:], in1=ne[:], op=ALU.mult)
+                nc.vector.tensor_tensor(out=ri[:], in0=ri[:], in1=zidx[:], op=ALU.add)
+                nc.vector.tensor_copy(out=idx[:, e, :], in_=ri[:])
+
+        tabs = ctx.enter_context(tc.tile_pool(name="tabs", bufs=1))
+        hold = ctx.enter_context(tc.tile_pool(name="hold", bufs=1))
+        f0p = ctx.enter_context(tc.tile_pool(name="f0p", bufs=3))
+        tsp = ctx.enter_context(tc.tile_pool(name="tsp", bufs=4))
+        gp = ctx.enter_context(tc.tile_pool(name="gp", bufs=2 * (LAG + 1)))
+        gmp = ctx.enter_context(tc.tile_pool(name="gmp", bufs=2))
+        o1p = ctx.enter_context(tc.tile_pool(name="o1p", bufs=2))
+
+        tbs = []
+        for r in range(NTB):
+            tb = tabs.tile([P, 5, 8, 128], F32, name="tb%d" % r)
+            nc.gpsimd.memset(tb[:], 0.0)
+            tbs.append(tb)
+
+        rows = [o.rearrange("b (x y) n -> (b x) (y n)", y=8)[0:PARK_ROWS, :] for o in (out_1, out_0)]
+        parkv = [r.rearrange("(r m) e -> r (m e)", m=12) for r in rows]
+        o0v = out_0.rearrange("b (s q u) t -> q b s u t", s=2, u=4)
+        o1v = out_1.rearrange("b (s q u) n -> q b s (u n)", s=2, u=4)
+
+        def conv(i, s):
+            y = ps_y.tile([P, 4, 128], F32, tag="y")
+            for u in range(4):
+                tau = 4 * s + u
+                nc.tensor.matmul_mx(
+                    out=y[:, u, :],
+                    lhsT=wcodes[:, tau * 128:(tau + 1) * 128].bitcast(FP8X4),
+                    lhsT_scale=wscales[:, tau * 128:(tau + 1) * 128],
+                    rhs=xcodes[:, i * 128:(i + 1) * 128].bitcast(FP8X4),
+                    rhs_scale=xscales[:, i * 128:(i + 1) * 128],
+                    start=True,
+                    stop=True,
+                )
+            return y
+
+        def pair_stats(i):
+            for s in range(2):
+                y = conv(i, s)
+                for u in range(4):
+                    for c in range(2):
+                        bp = 2 * i + c
+                        nc.vector.bn_stats(
+                            out=stats[:, 4 * s + u, 2 * bp:2 * bp + 2, :].rearrange("p i f -> p (i f)"),
+                            in_=y[:, u, c * 64:(c + 1) * 64],
+                        )
+
+        def group_affine(p0, p1):
+            b0, b1 = 2 * p0, 2 * p1
+            nb = b1 - b0
+            mp = small.tile([P, 8, 2 * nb], F32, tag="mp")
+            for tau in range(8):
+                nc.vector.tensor_scalar(
+                    out=mp[:, tau, :], in0=stats[:, tau, 2 * b0:2 * b1, 1], scalar1=pv[:, 0, tau:tau + 1],
+                    scalar2=None, op0=ALU.add,
+                )
+            sq = small.tile([P, 8, 2 * nb], F32, tag="sq")
+            nc.vector.tensor_tensor(out=sq[:], in0=mp[:], in1=mp[:], op=ALU.mult)
+            v2 = small.tile([P, 8, 2 * nb], F32, tag="v2")
+            nc.vector.scalar_tensor_tensor(
+                out=v2[:], in0=stats[:, :, 2 * b0:2 * b1, 2], scalar=1.0 / 32.0, in1=sq[:],
+                op0=ALU.mult, op1=ALU.add,
+            )
+            rs = small.tile([P, 2, 2, nb], F32, tag="rs")
+            for s in range(2):
+                for a, src in enumerate((mp, v2)):
+                    nc.vector.tensor_reduce(
+                        out=rs[:, a, s, :],
+                        in_=src[:, 4 * s:4 * s + 4, :].rearrange("p u (b i) -> p b u i", i=2),
+                        axis=AX.XY, op=ALU.add,
+                    )
+            pst = ps_st.tile([P, 4 * nb], F32, tag="pst")
+            nc.tensor.matmul(
+                out=pst[:], lhsT=ones8[:], rhs=rs[:].rearrange("p a s b -> p (a s b)"), start=True, stop=True
+            )
+            mu = small.tile([P, 2 * nb], F32, tag="mu")
+            nc.vector.tensor_scalar(out=mu[:], in0=pst[:, 0:2 * nb], scalar1=1.0 / 64.0, scalar2=None, op0=ALU.mult)
+            msq = small.tile([P, 2 * nb], F32, tag="msq")
+            nc.vector.tensor_tensor(out=msq[:], in0=mu[:], in1=mu[:], op=ALU.mult)
+            var = small.tile([P, 2 * nb], F32, tag="var")
+            nc.vector.scalar_tensor_tensor(
+                out=var[:], in0=pst[:, 2 * nb:4 * nb], scalar=1.0 / 64.0, in1=msq[:], op0=ALU.mult, op1=ALU.subtract
+            )
+            nc.vector.tensor_scalar(out=var[:], in0=var[:], scalar1=EPS, scalar2=None, op0=ALU.add)
+            sd = small.tile([P, 2 * nb], F32, tag="sd")
+            nc.scalar.activation(out=sd[:], in_=var[:], func=ACT.Sqrt)
+            rstd = small.tile([P, 2 * nb], F32, tag="rstd")
+            nc.vector.reciprocal(out=rstd[:], in_=sd[:])
+            for tau in range(8):
+                s = tau // 4
+                nc.vector.tensor_scalar(
+                    out=gain[:, tau, b0:b1], in0=rstd[:, s * nb:(s + 1) * nb], scalar1=pv[:, 1, tau:tau + 1],
+                    scalar2=None, op0=ALU.mult,
+                )
+                t1 = small.tile([P, nb], F32, tag="t1")
+                nc.vector.scalar_tensor_tensor(
+                    out=t1[:], in0=mu[:, s * nb:(s + 1) * nb], scalar=pv[:, 0, tau:tau + 1],
+                    in1=gain[:, tau, b0:b1], op0=ALU.subtract, op1=ALU.mult,
+                )
+                nc.vector.tensor_scalar(
+                    out=shift[:, tau, b0:b1], in0=t1[:], scalar1=-1.0, scalar2=pv[:, 2, tau:tau + 1],
+                    op0=ALU.mult, op1=ALU.add,
+                )
+
+        def store_out0(i, f0):
+            for c in range(2):
+                b = (2 * (i + ROT) + c) % NB
+                for s in range(2):
+                    nc.sync.dma_start(out=o0v[:, b, s, :, :], in_=f0[:, 4 * s:4 * s + 4, c * 64:(c + 1) * 64])
+
+        def store_out1(i, o1):
+            for c in range(2):
+                b = (2 * (i + ROT) + c) % NB
+                nc.sync.dma_start(out=o1v[:, b, :, :], in_=o1[:, c, :, :, :].rearrange("q s u n -> q s (u n)"))
+
+        held = []
+        gathered = {}
+
+        def front(i):
+            late = i >= NPAIR - NHOLD
+            if late:
+                f0 = hold.tile([P, 8, 128], F32, name="f0h%d" % i)
+            else:
+                f0 = f0p.tile([P, 8, 128], F32, tag="f0")
+            for s in range(2):
+                y = conv(i, s)
+                for u in range(4):
+                    tau = 4 * s + u
+                    for c in range(2):
+                        bp = 2 * i + c
+                        nc.scalar.activation(
+                            out=f0[:, tau, c * 64:(c + 1) * 64], in_=y[:, u, c * 64:(c + 1) * 64], func=ACT.Relu,
+                            bias=shift[:, tau, bp:bp + 1], scale=gain[:, tau, bp:bp + 1],
+                        )
+            if not late:
+                store_out0(i, f0)
+            tb = tbs[i % NTB]
+            prev = f0[:].rearrange("p a (c t) -> p (a c) t", t=64)
+            for k in range(1, 6):
+                wd = 1 << (k - 1)
+                nv = 65 - (1 << k)
+                cur = tb[:, k - 1, :, :].rearrange("p a (c t) -> p (a c) t", t=64)
+                nc.vector.tensor_tensor(
+                    out=cur[:, :, 0:nv], in0=prev[:, :, 0:nv], in1=prev[:, :, wd:wd + nv], op=ALU.max
+                )
+                prev = cur
+            area = i % 2
+            for kk in range(3):
+                tsb = tsp.tile([P, 2, 2, 512], F32, tag="tsb")
+                for kl in range(2):
+                    k = 2 * kk + kl
+                    for s in range(2):
+                        tp = ps_tp.tile([P, 4, 128], F32, tag="tp")
+                        for u in range(4):
+                            tau = 4 * s + u
+                            src = f0[:, tau, :] if k == 0 else tb[:, k - 1, tau, :]
+                            nc.tensor.transpose(tp[:, u, :], src, ident[:])
+                        nc.scalar.copy(out=tsb[:, kl, s, :], in_=tp[:].rearrange("p u q -> p (u q)"))
+                nc.sync.dma_start(
+                    out=parkv[area][:, kk * 2048:(kk + 1) * 2048], in_=tsb[:].rearrange("p k s e -> p (k s e)")
+                )
+            got = []
+            for s in range(2):
+                col = 2 * ((i + ROT) % NPAIR) + s
+                pairg = []
+                for e in range(2):
+                    g = gp.tile([P, 512], F32, tag="g%d" % e)
+                    nc.gpsimd.indirect_dma_start(
+                        out=g[:], out_offset=None, in_=rows[area],
+                        in_offset=bass.IndirectOffsetOnAxis(ap=idx[:, e, col:col + 1], axis=0),
+                    )
+                    pairg.append(g)
+                got.append(pairg)
+            gathered[i] = got
+            if late:
+                held.append((i, f0))
+
+        held1 = []
+
+        def back(i):
+            late = i >= NPAIR - NHOLD
+            if late:
+                o1 = hold.tile([P, 2, 2, 4, 64], F32, name="o1h%d" % i)
+            else:
+                o1 = o1p.tile([P, 2, 2, 4, 64], F32, tag="o1")
+            for s in range(2):
+                ga, ge = gathered[i][s]
+                gm = gmp.tile([P, 512], F32, tag="gm")
+                nc.vector.tensor_tensor(out=gm[:], in0=ga[:], in1=ge[:], op=ALU.max)
+                bk = ps_bk.tile([P, 4, 128], F32, tag="bk")
+                for u in range(4):
+                    nc.tensor.transpose(bk[:, u, :], gm[:, u * 128:(u + 1) * 128], ident[:])
+                nc.vector.tensor_copy(out=o1[:, :, s, :, :], in_=bk[:].rearrange("q u (c n) -> q c u n", c=2))
+            if late:
+                held1.append((i, o1))
+            else:
+                store_out1(i, o1)
+
+        done = [0, 0]
+
+        def advance(target):
+            while done[0] < target:
+                pair_stats(done[0])
+                done[0] += 1
+                if done[0] == STAT_GROUPS[done[1]][1]:
+                    group_affine(STAT_GROUPS[done[1]][0], STAT_GROUPS[done[1]][1])
+                    done[1] += 1
+
+        for j in range(NPAIR + LAG):
+            if j < NPAIR:
+                need = [g1 for g0, g1 in STAT_GROUPS if g0 <= j < g1][0]
+                advance(min(NPAIR, max(need, 2 * j + 4)))
+                front(j)
+            if j >= LAG:
+                back(j - LAG)
+        for i, f0 in held:
+            store_out0(i, f0)
+        for i, o1 in held1:
+            store_out1(i, o1)

@@ -20,13 +20,22 @@ FLOPS = 2 * 48 * 1024 * 512 * 64
 P = 128
 NB = 48
 NPAIR = 24
-ROT = 6
-NHOLD = 6
-PARK_ROWS = 1536
+ROT = 5
+NHOLD = 5
+PARK_ROWS = 1280
+WID = (1, 3, 6, 12, 24, 48)
+NV = (64, 62, 59, 53, 41, 17)
+OFF = (0, 128, 252, 370, 476, 558)
+NENT = 640
+ZERO0 = 592
 EPS = 1e-5
-LAG = 2
+LAG = 3
 NTB = 2
-STAT_GROUPS = ((0, 2), (2, 6), (6, 12), (12, 18), (18, 24))
+STAT_GROUPS = ((0, 1), (1, 3), (3, 7), (7, 12), (12, 18), (18, 24))
+BYTE_LOADS = ((0, 4), (4, 16), (16, 32), (32, 38), (38, 48))
+FEAT_CHUNKS = ((0, 2), (2, 4), (4, 8), (8, 16), (16, 24), (24, 32), (32, 40), (40, 48))
+HEAD_STEPS = 2
+SPLIT_STEP = 14
 
 
 def tile_coarsepyramid_pa_kernel(
@@ -40,6 +49,12 @@ def tile_coarsepyramid_pa_kernel(
         ps_tp = ctx.enter_context(tc.psum_pool(name="ps_tp", bufs=3))
         ps_bk = ctx.enter_context(tc.psum_pool(name="ps_bk", bufs=1))
         ps_st = ctx.enter_context(tc.psum_pool(name="ps_st", bufs=1))
+        tabs = ctx.enter_context(tc.tile_pool(name="tabs", bufs=1))
+        fsp = ctx.enter_context(tc.tile_pool(name="fsp", bufs=4))
+        m2p = ctx.enter_context(tc.tile_pool(name="m2p", bufs=1))
+        tsp = ctx.enter_context(tc.tile_pool(name="tsp", bufs=5))
+        gp = ctx.enter_context(tc.tile_pool(name="gp", bufs=2 * (LAG + 1)))
+        o1p = ctx.enter_context(tc.tile_pool(name="o1p", bufs=4))
 
         ident = const.tile([P, P], F32)
         make_identity(nc, ident[:])
@@ -54,158 +69,21 @@ def tile_coarsepyramid_pa_kernel(
         gain = const.tile([P, 8, NB], F32)
         shift = const.tile([P, 8, NB], F32)
         idx = const.tile([P, 2, 48], I32)
-        pv = const.tile([P, 3, 8], F32)
+        pv = const.tile([P, 3, 2, 4, 1], F32)
         sc = const.tile([P, 4], F32)
-
-        with tc.tile_pool(name="prep", bufs=1) as prep, tc.tile_pool(name="prep2", bufs=2) as prep2:
-            xb = prep.tile([P, NB, 256], U8)
-            fv = feature_bytes.rearrange("b (p j) t -> p b (j t)", j=4)
-            nc.sync.dma_start(out=sc[:], in_=feature_scale.rearrange("o (p j) i -> p (o j i)", j=4))
-            w_sb = prep.tile([P, 2, 4, 512], BF16)
-
-            def load_bytes(p0, p1):
-                b0 = (p0 + 2 * ROT) % NB
-                nc.sync.dma_start(out=xb[:, p0:p1, :], in_=fv[:, b0:b0 + (p1 - p0), :])
-
-            load_bytes(0, 4)
-            nc.sync.dma_start(
-                out=w_sb[:].rearrange("q s u k -> q s (u k)"),
-                in_=w_lr.rearrange("(s q u) k -> q s (u k)", s=2, u=4),
-            )
-            for p0, p1 in ((4, 8), (8, 16), (16, 32), (32, 36), (36, 48)):
-                load_bytes(p0, p1)
-
-            pv_bf = prep.tile([P, 3, 16], BF16)
-            for m, vec in enumerate((b_lr, g_lr, be_lr)):
-                nc.scalar.dma_start(
-                    out=pv_bf[:, m, 0:8].rearrange("q (s u) -> q s u", s=2),
-                    in_=vec.rearrange("(s q u) -> q s u", s=2, u=4),
-                )
-            sg_bf = prep.tile([P, NPAIR, 4], BF16)
-            seg_v = segments.rearrange("(i c) n f -> c n i f", c=2)
-            for c in range(2):
-                nc.scalar.dma_start(out=sg_bf[c * 64:(c + 1) * 64, :, :], in_=seg_v[c])
-            nc.vector.tensor_copy(out=pv[:], in_=pv_bf[:, :, 0:8])
-
-            wg = prep.tile([P, 8, 128, 4], BF16, align_bytes=64)
-            for h in range(4):
-                xt = ps_tp.tile([P, 2, 2, 128], F32, tag="tp")
-                for a in range(2):
-                    tau = 2 * h + a
-                    words = w_sb[:, tau // 4, tau % 4, :].bitcast(F32)
-                    for v in range(2):
-                        nc.tensor.transpose(xt[:, a, v, :], words[:, v:256:2], ident[:])
-                nc.vector.tensor_copy(
-                    out=wg[:, 2 * h:2 * h + 2, :, :].rearrange("p a q e -> p a (q e)").bitcast(F32)
-                    .rearrange("p a (q v) -> p a q v", v=2),
-                    in_=xt[:].rearrange("p a v q -> p a q v"),
-                )
-            nc.vector.quantize_mx(
-                out=wcodes[:].bitcast(FP8X4), scales=wscales[:], in_=wg[:].rearrange("p a q e -> p (a q e)")
-            )
-
-            for ci, (p0, p1) in enumerate(((0, 4), (4, 8), (8, 16), (16, 32), (32, 48))):
-                n = p1 - p0
-                xc = prep2.tile([P, n * 256], BF16, tag="xc")
-                nc.scalar.copy(out=xc[:], in_=xb[:, p0:p1, :].rearrange("p b e -> p (b e)").bitcast(FP8))
-                gx = prep2.tile([P, n * 64, 4], BF16, tag="gx", align_bytes=64)
-                xc4 = xc[:].rearrange("p (b j t) -> p b j t", j=4, t=64)
-                gx4 = gx[:].rearrange("p (b t) j -> p b t j", t=64)
-                for j in range(4):
-                    if ci < 2:
-                        nc.vector.tensor_scalar(
-                            out=gx4[:, :, :, j], in0=xc4[:, :, j, :], scalar1=sc[:, j:j + 1], scalar2=None,
-                            op0=ALU.mult,
-                        )
-                    else:
-                        nc.gpsimd.tensor_scalar(
-                            out=gx4[:, :, :, j], in0=xc4[:, :, j, :], scalar1=sc[:, j:j + 1], scalar2=0.0,
-                            op0=ALU.mult, op1=ALU.add,
-                        )
-                nc.vector.quantize_mx(
-                    out=xcodes[:, p0 * 64:p1 * 64].bitcast(FP8X4),
-                    scales=xscales[:, p0 * 64:p1 * 64],
-                    in_=gx[:].rearrange("p c j -> p (c j)"),
-                )
-
-            xs = prep.tile([P, 96], F32)
-            nc.vector.tensor_scalar(
-                out=xs[:], in0=sg_bf[:].rearrange("p i f -> p (i f)"), scalar1=0.0, scalar2=63.0,
-                op0=ALU.max, op1=ALU.min,
-            )
-            xi = prep.tile([P, 96], I32)
-            nc.vector.tensor_copy(out=xi[:], in_=xs[:])
-            xf = prep.tile([P, 96], F32)
-            nc.vector.tensor_copy(out=xf[:], in_=xi[:])
-            gt = prep.tile([P, 96], F32)
-            nc.vector.tensor_tensor(out=gt[:], in0=xf[:], in1=xs[:], op=ALU.is_gt)
-            fl = prep.tile([P, 48, 2], F32)
-            nc.vector.tensor_tensor(out=fl[:].rearrange("p c e -> p (c e)"), in0=xf[:], in1=gt[:], op=ALU.subtract)
-            lo = fl[:, :, 0]
-            hi = fl[:, :, 1]
-            lm = prep.tile([P, 48], F32)
-            nc.vector.tensor_tensor(out=lm[:], in0=hi, in1=lo, op=ALU.subtract)
-            fk = prep.tile([P, 48, 5], F32)
-            fw = prep.tile([P, 48, 5], F32)
-            for j in range(1, 6):
-                thr = float(2 ** j - 1)
-                nc.vector.tensor_scalar(
-                    out=fk[:, :, j - 1], in0=lm[:], scalar1=thr, scalar2=2.0, op0=ALU.is_ge, op1=ALU.mult
-                )
-                nc.vector.tensor_scalar(
-                    out=fw[:, :, j - 1], in0=lm[:], scalar1=thr, scalar2=float(2 - 6 * 2 ** j),
-                    op0=ALU.is_ge, op1=ALU.mult,
-                )
-            k2 = prep.tile([P, 48], F32)
-            nc.vector.tensor_reduce(out=k2[:], in_=fk[:], axis=AX.X, op=ALU.add)
-            ue = prep.tile([P, 48], F32)
-            nc.vector.tensor_reduce(out=ue[:], in_=fw[:], axis=AX.X, op=ALU.add)
-            b12i = prep.tile([P, 48], I32)
-            for c in range(2):
-                nc.gpsimd.iota(
-                    b12i[c * 64:(c + 1) * 64, :], pattern=[[0, 24], [1, 2]], base=768 * c, channel_multiplier=0
-                )
-            b12 = prep.tile([P, 48], F32)
-            nc.vector.tensor_copy(out=b12[:], in_=b12i[:])
-            pidx = prep.tile([P, 1], I32)
-            nc.gpsimd.iota(pidx[:], pattern=[[0, 1]], base=0, channel_multiplier=1)
-            pand = prep.tile([P, 1], I32)
-            nc.vector.tensor_single_scalar(out=pand[:], in_=pidx[:], scalar=15, op=ALU.bitwise_and)
-            pf = prep.tile([P, 1], F32)
-            nc.vector.tensor_copy(out=pf[:], in_=pand[:])
-            zc = prep.tile([P, 1], F32)
-            nc.vector.tensor_scalar(out=zc[:], in0=pf[:], scalar1=12.0, scalar2=586.0, op0=ALU.mult, op1=ALU.add)
-            zidx = prep.tile([P, 48], F32)
-            nc.vector.tensor_scalar(out=zidx[:], in0=b12[:], scalar1=zc[:, 0:1], scalar2=None, op0=ALU.add)
-            for e, (pos, extra, thr) in enumerate(((lo, k2, 0.0), (hi, ue, 1.0))):
-                ri = prep.tile([P, 48], F32, name="ri%d" % e)
-                nc.vector.scalar_tensor_tensor(out=ri[:], in0=pos, scalar=12.0, in1=b12[:], op0=ALU.mult, op1=ALU.add)
-                nc.vector.tensor_tensor(out=ri[:], in0=ri[:], in1=extra[:], op=ALU.add)
-                nc.vector.tensor_tensor(out=ri[:], in0=ri[:], in1=zidx[:], op=ALU.subtract)
-                ne = prep.tile([P, 48], F32, name="ne%d" % e)
-                nc.vector.tensor_single_scalar(out=ne[:], in_=lm[:], scalar=thr, op=ALU.is_ge)
-                nc.vector.tensor_tensor(out=ri[:], in0=ri[:], in1=ne[:], op=ALU.mult)
-                nc.vector.tensor_tensor(out=ri[:], in0=ri[:], in1=zidx[:], op=ALU.add)
-                nc.vector.tensor_copy(out=idx[:, e, :], in_=ri[:])
-
-        tabs = ctx.enter_context(tc.tile_pool(name="tabs", bufs=1))
-        hold = ctx.enter_context(tc.tile_pool(name="hold", bufs=1))
-        f0p = ctx.enter_context(tc.tile_pool(name="f0p", bufs=3))
-        tsp = ctx.enter_context(tc.tile_pool(name="tsp", bufs=4))
-        gp = ctx.enter_context(tc.tile_pool(name="gp", bufs=2 * (LAG + 1)))
-        gmp = ctx.enter_context(tc.tile_pool(name="gmp", bufs=2))
-        o1p = ctx.enter_context(tc.tile_pool(name="o1p", bufs=2))
+        warm = const.tile([P, 2], F32)
+        nc.gpsimd.memset(warm[:], 1.0)
 
         tbs = []
         for r in range(NTB):
-            tb = tabs.tile([P, 5, 8, 128], F32, name="tb%d" % r)
+            tb = tabs.tile([P, 8, NENT], F32, name="tb%d" % r)
             nc.gpsimd.memset(tb[:], 0.0)
             tbs.append(tb)
 
         rows = [o.rearrange("b (x y) n -> (b x) (y n)", y=8)[0:PARK_ROWS, :] for o in (out_1, out_0)]
-        parkv = [r.rearrange("(r m) e -> r (m e)", m=12) for r in rows]
-        o0v = out_0.rearrange("b (s q u) t -> q b s u t", s=2, u=4)
-        o1v = out_1.rearrange("b (s q u) n -> q b s (u n)", s=2, u=4)
+        parkv = [r.rearrange("(r p s) e -> p r (s e)", p=P, s=2) for r in rows]
+        o0v = out_0.rearrange("b (s q u) t -> q (b s) (u t)", s=2, u=4)
+        o1v = out_1.rearrange("b (s q u) n -> q (b s) (u n)", s=2, u=4)
 
         def conv(i, s):
             y = ps_y.tile([P, 4, 128], F32, tag="y")
@@ -236,12 +114,14 @@ def tile_coarsepyramid_pa_kernel(
         def group_affine(p0, p1):
             b0, b1 = 2 * p0, 2 * p1
             nb = b1 - b0
+            bias_c = pv[:, 0, :, :, :]
+            g_c = pv[:, 1, :, :, :]
+            be_c = pv[:, 2, :, :, :]
             mp = small.tile([P, 8, 2 * nb], F32, tag="mp")
-            for tau in range(8):
-                nc.vector.tensor_scalar(
-                    out=mp[:, tau, :], in0=stats[:, tau, 2 * b0:2 * b1, 1], scalar1=pv[:, 0, tau:tau + 1],
-                    scalar2=None, op0=ALU.add,
-                )
+            nc.vector.tensor_tensor(
+                out=mp[:], in0=stats[:, :, 2 * b0:2 * b1, 1],
+                in1=bias_c.rearrange("p s u o -> p (s u) o").to_broadcast([P, 8, 2 * nb]), op=ALU.add,
+            )
             sq = small.tile([P, 8, 2 * nb], F32, tag="sq")
             nc.vector.tensor_tensor(out=sq[:], in0=mp[:], in1=mp[:], op=ALU.mult)
             v2 = small.tile([P, 8, 2 * nb], F32, tag="v2")
@@ -261,10 +141,11 @@ def tile_coarsepyramid_pa_kernel(
             nc.tensor.matmul(
                 out=pst[:], lhsT=ones8[:], rhs=rs[:].rearrange("p a s b -> p (a s b)"), start=True, stop=True
             )
-            mu = small.tile([P, 2 * nb], F32, tag="mu")
-            nc.vector.tensor_scalar(out=mu[:], in0=pst[:, 0:2 * nb], scalar1=1.0 / 64.0, scalar2=None, op0=ALU.mult)
+            mu = small.tile([P, 2, 1, nb], F32, tag="mu")
+            muf = mu[:].rearrange("p s o b -> p (s o b)")
+            nc.vector.tensor_scalar(out=muf, in0=pst[:, 0:2 * nb], scalar1=1.0 / 64.0, scalar2=None, op0=ALU.mult)
             msq = small.tile([P, 2 * nb], F32, tag="msq")
-            nc.vector.tensor_tensor(out=msq[:], in0=mu[:], in1=mu[:], op=ALU.mult)
+            nc.vector.tensor_tensor(out=msq[:], in0=muf, in1=muf, op=ALU.mult)
             var = small.tile([P, 2 * nb], F32, tag="var")
             nc.vector.scalar_tensor_tensor(
                 out=var[:], in0=pst[:, 2 * nb:4 * nb], scalar=1.0 / 64.0, in1=msq[:], op0=ALU.mult, op1=ALU.subtract
@@ -272,44 +153,46 @@ def tile_coarsepyramid_pa_kernel(
             nc.vector.tensor_scalar(out=var[:], in0=var[:], scalar1=EPS, scalar2=None, op0=ALU.add)
             sd = small.tile([P, 2 * nb], F32, tag="sd")
             nc.scalar.activation(out=sd[:], in_=var[:], func=ACT.Sqrt)
-            rstd = small.tile([P, 2 * nb], F32, tag="rstd")
-            nc.vector.reciprocal(out=rstd[:], in_=sd[:])
-            for tau in range(8):
-                s = tau // 4
-                nc.vector.tensor_scalar(
-                    out=gain[:, tau, b0:b1], in0=rstd[:, s * nb:(s + 1) * nb], scalar1=pv[:, 1, tau:tau + 1],
-                    scalar2=None, op0=ALU.mult,
-                )
-                t1 = small.tile([P, nb], F32, tag="t1")
-                nc.vector.scalar_tensor_tensor(
-                    out=t1[:], in0=mu[:, s * nb:(s + 1) * nb], scalar=pv[:, 0, tau:tau + 1],
-                    in1=gain[:, tau, b0:b1], op0=ALU.subtract, op1=ALU.mult,
-                )
-                nc.vector.tensor_scalar(
-                    out=shift[:, tau, b0:b1], in0=t1[:], scalar1=-1.0, scalar2=pv[:, 2, tau:tau + 1],
-                    op0=ALU.mult, op1=ALU.add,
-                )
+            rstd = small.tile([P, 2, 1, nb], F32, tag="rstd")
+            nc.vector.reciprocal(out=rstd[:].rearrange("p s o b -> p (s o b)"), in_=sd[:])
+            full = [P, 2, 4, nb]
+            gn = gain[:, :, b0:b1].rearrange("p (s u) b -> p s u b", s=2)
+            sh = shift[:, :, b0:b1].rearrange("p (s u) b -> p s u b", s=2)
+            nc.vector.tensor_tensor(out=gn, in0=rstd[:].to_broadcast(full), in1=g_c.to_broadcast(full), op=ALU.mult)
+            t1 = small.tile([P, 2, 4, nb], F32, tag="t1")
+            nc.vector.tensor_tensor(
+                out=t1[:], in0=bias_c.to_broadcast(full), in1=mu[:].to_broadcast(full), op=ALU.subtract
+            )
+            nc.vector.tensor_tensor(out=t1[:], in0=t1[:], in1=gn, op=ALU.mult)
+            nc.vector.tensor_tensor(out=sh, in0=t1[:], in1=be_c.to_broadcast(full), op=ALU.add)
 
-        def store_out0(i, f0):
-            for c in range(2):
-                b = (2 * (i + ROT) + c) % NB
-                for s in range(2):
-                    nc.sync.dma_start(out=o0v[:, b, s, :, :], in_=f0[:, 4 * s:4 * s + 4, c * 64:(c + 1) * 64])
+        def store_out0(i, fs):
+            b0 = (2 * (i + ROT)) % NB
+            nc.sync.dma_start(
+                out=o0v[:, 2 * b0:2 * b0 + 4, :], in_=fs[:].rearrange("q c (s u) t -> q (c s) (u t)", s=2)
+            )
 
         def store_out1(i, o1):
-            for c in range(2):
-                b = (2 * (i + ROT) + c) % NB
-                nc.sync.dma_start(out=o1v[:, b, :, :], in_=o1[:, c, :, :, :].rearrange("q s u n -> q s (u n)"))
+            b0 = (2 * (i + ROT)) % NB
+            nc.sync.dma_start(out=o1v[:, 2 * b0:2 * b0 + 4, :], in_=o1[:].rearrange("q c s u n -> q (c s) (u n)"))
 
-        held = []
+        pending = [[], []]
+
+        def flush(area):
+            for i, t in pending[area]:
+                if area == 0:
+                    store_out1(i, t)
+                else:
+                    store_out0(i, t)
+            pending[area].clear()
+
+        held0 = []
+        held1 = []
         gathered = {}
+        pools = {}
 
-        def front(i):
-            late = i >= NPAIR - NHOLD
-            if late:
-                f0 = hold.tile([P, 8, 128], F32, name="f0h%d" % i)
-            else:
-                f0 = f0p.tile([P, 8, 128], F32, tag="f0")
+        def front_a(i):
+            tb = tbs[i % NTB]
             for s in range(2):
                 y = conv(i, s)
                 for u in range(4):
@@ -317,36 +200,51 @@ def tile_coarsepyramid_pa_kernel(
                     for c in range(2):
                         bp = 2 * i + c
                         nc.scalar.activation(
-                            out=f0[:, tau, c * 64:(c + 1) * 64], in_=y[:, u, c * 64:(c + 1) * 64], func=ACT.Relu,
+                            out=tb[:, tau, c * 64:(c + 1) * 64], in_=y[:, u, c * 64:(c + 1) * 64], func=ACT.Relu,
                             bias=shift[:, tau, bp:bp + 1], scale=gain[:, tau, bp:bp + 1],
                         )
-            if not late:
-                store_out0(i, f0)
-            tb = tbs[i % NTB]
-            prev = f0[:].rearrange("p a (c t) -> p (a c) t", t=64)
-            for k in range(1, 6):
-                wd = 1 << (k - 1)
-                nv = 65 - (1 << k)
-                cur = tb[:, k - 1, :, :].rearrange("p a (c t) -> p (a c) t", t=64)
+            return tb
+
+        def level(tb, k):
+            return tb[:, :, OFF[k]:OFF[k] + 2 * NV[k]].rearrange("p a (c t) -> p a c t", c=2)
+
+        def front_b(i, tb, after_tables):
+            f = level(tb, 0)
+            m2 = m2p.tile([P, 8, 2, 63], F32, tag="m2")
+            nc.vector.tensor_tensor(out=m2[:], in0=f[:, :, :, 0:63], in1=f[:, :, :, 1:64], op=ALU.max)
+            nc.vector.tensor_tensor(out=level(tb, 1), in0=m2[:, :, :, 0:62], in1=m2[:, :, :, 1:63], op=ALU.max)
+            for k in range(2, 6):
+                prev = level(tb, k - 1)
                 nc.vector.tensor_tensor(
-                    out=cur[:, :, 0:nv], in0=prev[:, :, 0:nv], in1=prev[:, :, wd:wd + nv], op=ALU.max
+                    out=level(tb, k), in0=prev[:, :, :, 0:NV[k]], in1=prev[:, :, :, WID[k - 1]:WID[k - 1] + NV[k]],
+                    op=ALU.max,
                 )
-                prev = cur
+            if after_tables is not None:
+                after_tables()
             area = i % 2
-            for kk in range(3):
+            for g in range(3):
+                nr = min(2, 5 - 2 * g)
                 tsb = tsp.tile([P, 2, 2, 512], F32, tag="tsb")
-                for kl in range(2):
-                    k = 2 * kk + kl
+                for rl in range(nr):
+                    r = 2 * g + rl
                     for s in range(2):
                         tp = ps_tp.tile([P, 4, 128], F32, tag="tp")
                         for u in range(4):
-                            tau = 4 * s + u
-                            src = f0[:, tau, :] if k == 0 else tb[:, k - 1, tau, :]
-                            nc.tensor.transpose(tp[:, u, :], src, ident[:])
-                        nc.scalar.copy(out=tsb[:, kl, s, :], in_=tp[:].rearrange("p u q -> p (u q)"))
+                            nc.tensor.transpose(tp[:, u, :], tb[:, 4 * s + u, r * 128:(r + 1) * 128], ident[:])
+                        nc.scalar.copy(out=tsb[:, rl, s, :], in_=tp[:].rearrange("p u q -> p (u q)"))
                 nc.sync.dma_start(
-                    out=parkv[area][:, kk * 2048:(kk + 1) * 2048], in_=tsb[:].rearrange("p k s e -> p (k s e)")
+                    out=parkv[area][:, 2 * g:2 * g + nr, :], in_=tsb[:, 0:nr, :, :].rearrange("p r s e -> p r (s e)")
                 )
+            late = i >= NPAIR - NHOLD
+            if late:
+                fs = pools["hold"].tile([P, 2, 8, 64], F32, name="fsh%d" % i)
+                held0.append((i, fs))
+            else:
+                fs = fsp.tile([P, 2, 8, 64], F32, tag="fs")
+                pending[1].append((i, fs))
+            for c in range(2):
+                nc.scalar.copy(out=fs[:, c, :, :], in_=tb[:, :, c * 64:(c + 1) * 64])
+            flush(area)
             got = []
             for s in range(2):
                 col = 2 * ((i + ROT) % NPAIR) + s
@@ -360,48 +258,218 @@ def tile_coarsepyramid_pa_kernel(
                     pairg.append(g)
                 got.append(pairg)
             gathered[i] = got
-            if late:
-                held.append((i, f0))
-
-        held1 = []
-
         def back(i):
             late = i >= NPAIR - NHOLD
             if late:
-                o1 = hold.tile([P, 2, 2, 4, 64], F32, name="o1h%d" % i)
+                o1 = pools["hold"].tile([P, 2, 2, 4, 64], F32, name="o1h%d" % i)
+                held1.append((i, o1))
             else:
                 o1 = o1p.tile([P, 2, 2, 4, 64], F32, tag="o1")
             for s in range(2):
                 ga, ge = gathered[i][s]
-                gm = gmp.tile([P, 512], F32, tag="gm")
-                nc.vector.tensor_tensor(out=gm[:], in0=ga[:], in1=ge[:], op=ALU.max)
+                nc.vector.tensor_tensor(out=ga[:], in0=ga[:], in1=ge[:], op=ALU.max)
+            for s in range(2):
+                ga, ge = gathered[i][s]
                 bk = ps_bk.tile([P, 4, 128], F32, tag="bk")
                 for u in range(4):
-                    nc.tensor.transpose(bk[:, u, :], gm[:, u * 128:(u + 1) * 128], ident[:])
+                    nc.tensor.transpose(bk[:, u, :], ga[:, u * 128:(u + 1) * 128], ident[:])
                 nc.vector.tensor_copy(out=o1[:, :, s, :, :], in_=bk[:].rearrange("q u (c n) -> q c u n", c=2))
-            if late:
-                held1.append((i, o1))
+            if not late:
+                pending[0].append((i, o1))
+
+        done = [0, 0, 0]
+
+        def features_for(npairs, feat_chunk):
+            while done[2] < len(FEAT_CHUNKS) and FEAT_CHUNKS[done[2]][0] < 2 * npairs:
+                feat_chunk(FEAT_CHUNKS[done[2]][0], FEAT_CHUNKS[done[2]][1])
+                done[2] += 1
+
+        def stats_one(feat_chunk):
+            features_for(done[0] + 1, feat_chunk)
+            pair_stats(done[0])
+            done[0] += 1
+            if done[0] == STAT_GROUPS[done[1]][1]:
+                group_affine(STAT_GROUPS[done[1]][0], STAT_GROUPS[done[1]][1])
+                done[1] += 1
+
+        def late_stores(j):
+            if j >= NPAIR - 2:
+                flush(0)
+                for i, o1 in held1:
+                    store_out1(i, o1)
+                held1.clear()
+            if j >= NPAIR - 1:
+                flush(1)
+                for i, f0 in held0:
+                    store_out0(i, f0)
+                held0.clear()
+
+        def activations(i, feat_chunk):
+            while done[1] < len(STAT_GROUPS) and STAT_GROUPS[done[1]][0] <= i:
+                stats_one(feat_chunk)
+            front_a(i)
+
+        def step(j, feat_chunk, after_tables):
+            ahead = min(NPAIR, 2 * j + 6)
+            if j == 0:
+                activations(0, feat_chunk)
+                front_b(0, tbs[0], after_tables)
+                activations(1, feat_chunk)
             else:
-                store_out1(i, o1)
-
-        done = [0, 0]
-
-        def advance(target):
-            while done[0] < target:
-                pair_stats(done[0])
-                done[0] += 1
-                if done[0] == STAT_GROUPS[done[1]][1]:
-                    group_affine(STAT_GROUPS[done[1]][0], STAT_GROUPS[done[1]][1])
-                    done[1] += 1
-
-        for j in range(NPAIR + LAG):
-            if j < NPAIR:
-                need = [g1 for g0, g1 in STAT_GROUPS if g0 <= j < g1][0]
-                advance(min(NPAIR, max(need, 2 * j + 4)))
-                front(j)
+                if j + 1 < NPAIR:
+                    activations(j + 1, feat_chunk)
+                if done[0] < ahead:
+                    stats_one(feat_chunk)
+                if j < NPAIR:
+                    front_b(j, tbs[j % NTB], after_tables)
             if j >= LAG:
                 back(j - LAG)
-        for i, f0 in held:
-            store_out0(i, f0)
-        for i, o1 in held1:
-            store_out1(i, o1)
+            late_stores(j)
+            while done[0] < ahead:
+                stats_one(feat_chunk)
+            features_for(min(NPAIR, 2 * j + 8), feat_chunk)
+
+        with tc.tile_pool(name="prep", bufs=1) as prep, tc.tile_pool(name="prep2", bufs=2) as prep2:
+            with tc.manual_schedule():
+                xb = prep.tile([P, 4, NB, 64], U8)
+                fv = feature_bytes.rearrange("b (p j) t -> j p b t", j=4)
+                w_sb = prep.tile([P, 2, 4, 512], BF16)
+                nc.sync.dma_start(out=sc[:], in_=feature_scale.rearrange("o (p j) i -> p (o j i)", j=4))
+                for li, (p0, p1) in enumerate(BYTE_LOADS):
+                    b0 = (p0 + 2 * ROT) % NB
+                    for j in range(4):
+                        nc.sync.dma_start(out=xb[:, j, p0:p1, :], in_=fv[j][:, b0:b0 + (p1 - p0), :])
+                    if li == 0:
+                        nc.sync.dma_start(
+                            out=w_sb[:].rearrange("q s u k -> q s (u k)"),
+                            in_=w_lr.rearrange("(s q u) k -> q s (u k)", s=2, u=4),
+                        )
+                pv_bf = prep.tile([P, 3, 16], BF16)
+                for m, vec in enumerate((b_lr, g_lr, be_lr)):
+                    nc.scalar.dma_start(
+                        out=pv_bf[:, m, 0:8].rearrange("q (s u) -> q s u", s=2),
+                        in_=vec.rearrange("(s q u) -> q s u", s=2, u=4),
+                    )
+                sg_bf = prep.tile([P, NPAIR, 4], BF16)
+                seg_v = segments.rearrange("(i c) n f -> c n i f", c=2)
+                for c in range(2):
+                    nc.scalar.dma_start(out=sg_bf[c * 64:(c + 1) * 64, :, :], in_=seg_v[c])
+                nc.scalar.activation(out=warm[:, 1:2], in_=warm[:, 0:1], func=ACT.Sqrt)
+                nc.vector.tensor_copy(out=pv[:].rearrange("p m s u o -> p m (s u o)"), in_=pv_bf[:, :, 0:8])
+
+                def feat_chunk(p0, p1):
+                    n = p1 - p0
+                    gx = prep2.tile([P, n * 64, 4], BF16, tag="gx", align_bytes=64)
+                    for j in range(4):
+                        nc.vector.tensor_scalar(
+                            out=gx[:, :, j], in0=xb[:, j, p0:p1, :].rearrange("p b t -> p (b t)").bitcast(FP8),
+                            scalar1=sc[:, j:j + 1], scalar2=None, op0=ALU.mult,
+                        )
+                    nc.vector.quantize_mx(
+                        out=xcodes[:, p0 * 64:p1 * 64].bitcast(FP8X4),
+                        scales=xscales[:, p0 * 64:p1 * 64],
+                        in_=gx[:].rearrange("p c j -> p (c j)"),
+                    )
+
+                features_for(2, feat_chunk)
+
+                wg = prep.tile([P, 8, 128, 4], BF16, align_bytes=64)
+                for h in range(4):
+                    xt = ps_tp.tile([P, 2, 2, 128], F32, tag="tp")
+                    for a in range(2):
+                        tau = 2 * h + a
+                        words = w_sb[:, tau // 4, tau % 4, :].bitcast(F32)
+                        for v in range(2):
+                            nc.tensor.transpose(xt[:, a, v, :], words[:, v:256:2], ident[:])
+                    nc.vector.tensor_copy(
+                        out=wg[:, 2 * h:2 * h + 2, :, :].rearrange("p a q e -> p a (q e)").bitcast(F32)
+                        .rearrange("p a (q v) -> p a q v", v=2),
+                        in_=xt[:].rearrange("p a v q -> p a q v"),
+                    )
+                nc.vector.quantize_mx(
+                    out=wcodes[:].bitcast(FP8X4), scales=wscales[:], in_=wg[:].rearrange("p a q e -> p (a q e)")
+                )
+
+                def row_indices():
+                    xs = prep.tile([P, 96], F32)
+                    nc.vector.tensor_scalar(
+                        out=xs[:], in0=sg_bf[:].rearrange("p i f -> p (i f)"), scalar1=0.0, scalar2=63.0,
+                        op0=ALU.max, op1=ALU.min,
+                    )
+                    xi = prep.tile([P, 96], I32)
+                    nc.vector.tensor_copy(out=xi[:], in_=xs[:])
+                    xf = prep.tile([P, 96], F32)
+                    nc.vector.tensor_copy(out=xf[:], in_=xi[:])
+                    gt = prep.tile([P, 96], F32)
+                    nc.vector.tensor_tensor(out=gt[:], in0=xf[:], in1=xs[:], op=ALU.is_gt)
+                    fl = prep.tile([P, 48, 2], F32)
+                    nc.vector.tensor_tensor(
+                        out=fl[:].rearrange("p c e -> p (c e)"), in0=xf[:], in1=gt[:], op=ALU.subtract
+                    )
+                    lo = fl[:, :, 0]
+                    hi = fl[:, :, 1]
+                    lm = prep.tile([P, 48], F32)
+                    nc.vector.tensor_tensor(out=lm[:], in0=hi, in1=lo, op=ALU.subtract)
+                    fa = prep.tile([P, 48, 5], F32)
+                    fd = prep.tile([P, 48, 5], F32)
+                    for j in range(1, 6):
+                        thr = float(WID[j] - 1)
+                        nc.vector.tensor_scalar(
+                            out=fa[:, :, j - 1], in0=lm[:], scalar1=thr, scalar2=float(4 * NV[j - 1]),
+                            op0=ALU.is_ge, op1=ALU.mult,
+                        )
+                        nc.vector.tensor_scalar(
+                            out=fd[:, :, j - 1], in0=lm[:], scalar1=thr, scalar2=float(2 * (WID[j] - WID[j - 1])),
+                            op0=ALU.is_ge, op1=ALU.mult,
+                        )
+                    sa = prep.tile([P, 48], F32)
+                    nc.vector.tensor_reduce(out=sa[:], in_=fa[:], axis=AX.X, op=ALU.add)
+                    sd2 = prep.tile([P, 48], F32)
+                    nc.vector.tensor_reduce(out=sd2[:], in_=fd[:], axis=AX.X, op=ALU.add)
+                    side_i = prep.tile([P, 48], I32)
+                    nc.gpsimd.iota(side_i[:], pattern=[[0, 24], [1, 2]], base=0, channel_multiplier=0)
+                    side = prep.tile([P, 48], F32)
+                    nc.vector.tensor_copy(out=side[:], in_=side_i[:])
+                    pidx = prep.tile([P, 1], I32)
+                    nc.gpsimd.iota(pidx[:], pattern=[[0, 1]], base=0, channel_multiplier=1)
+                    pint = prep.tile([P, 2], I32)
+                    nc.vector.tensor_single_scalar(out=pint[:, 0:1], in_=pidx[:], scalar=6, op=ALU.logical_shift_right)
+                    nc.vector.tensor_single_scalar(out=pint[:, 1:2], in_=pidx[:], scalar=31, op=ALU.bitwise_and)
+                    pfl = prep.tile([P, 2], F32)
+                    nc.vector.tensor_copy(out=pfl[:], in_=pint[:])
+                    c128 = prep.tile([P, 1], F32)
+                    nc.vector.tensor_scalar(out=c128[:], in0=pfl[:, 0:1], scalar1=128.0, scalar2=None, op0=ALU.mult)
+                    zc = prep.tile([P, 1], F32)
+                    nc.vector.tensor_scalar(
+                        out=zc[:], in0=pfl[:, 1:2], scalar1=2.0, scalar2=float(2 * ZERO0), op0=ALU.mult, op1=ALU.add
+                    )
+                    zidx = prep.tile([P, 48], F32)
+                    nc.vector.tensor_scalar(out=zidx[:], in0=side[:], scalar1=zc[:, 0:1], scalar2=None, op0=ALU.add)
+                    cd = prep.tile([P, 48], F32)
+                    nc.vector.tensor_scalar(out=cd[:], in0=sd2[:], scalar1=pfl[:, 0:1], scalar2=None, op0=ALU.mult)
+                    com = prep.tile([P, 48], F32)
+                    nc.vector.tensor_tensor(out=com[:], in0=sa[:], in1=cd[:], op=ALU.subtract)
+                    nc.vector.tensor_tensor(out=com[:], in0=com[:], in1=side[:], op=ALU.add)
+                    nc.vector.tensor_scalar(out=com[:], in0=com[:], scalar1=c128[:, 0:1], scalar2=None, op0=ALU.add)
+                    for e, (pos, thr) in enumerate(((lo, 0.0), (hi, 1.0))):
+                        ri = prep.tile([P, 48], F32, name="ri%d" % e)
+                        nc.vector.scalar_tensor_tensor(
+                            out=ri[:], in0=pos, scalar=2.0, in1=com[:], op0=ALU.mult, op1=ALU.add
+                        )
+                        if e == 1:
+                            nc.vector.tensor_tensor(out=ri[:], in0=ri[:], in1=sd2[:], op=ALU.subtract)
+                        nc.vector.tensor_tensor(out=ri[:], in0=ri[:], in1=zidx[:], op=ALU.subtract)
+                        ne = prep.tile([P, 48], F32, name="ne%d" % e)
+                        nc.vector.tensor_single_scalar(out=ne[:], in_=lm[:], scalar=thr, op=ALU.is_ge)
+                        nc.vector.tensor_tensor(out=ri[:], in0=ri[:], in1=ne[:], op=ALU.mult)
+                        nc.vector.tensor_tensor(out=ri[:], in0=ri[:], in1=zidx[:], op=ALU.add)
+                        nc.vector.tensor_copy(out=idx[:, e, :], in_=ri[:])
+
+                for j in range(HEAD_STEPS):
+                    step(j, feat_chunk, row_indices if j == 0 else None)
+            for j in range(HEAD_STEPS, SPLIT_STEP):
+                step(j, feat_chunk, None)
+
+        pools["hold"] = ctx.enter_context(tc.tile_pool(name="hold", bufs=1))
+        for j in range(SPLIT_STEP, NPAIR + LAG):
+            step(j, None, None)

@@ -31,11 +31,11 @@ ZERO0 = 592
 EPS = 1e-5
 LAG = 3
 NTB = 2
-STAT_GROUPS = ((0, 1), (1, 3), (3, 7), (7, 12), (12, 18), (18, 24))
+STAT_GROUPS = ((0, 1), (1, 3), (3, 6), (6, 9), (9, 12), (12, 15), (15, 18), (18, 21), (21, 24))
 BYTE_LOADS = ((0, 4), (4, 16), (16, 32), (32, 38), (38, 48))
-FEAT_CHUNKS = ((0, 2), (2, 4), (4, 8), (8, 16), (16, 24), (24, 32), (32, 40), (40, 48))
+FEAT_CHUNKS = ((0, 2), (2, 4), (4, 8), (8, 12), (12, 16), (16, 20), (20, 24), (24, 28), (28, 32), (32, 36), (36, 40), (40, 44), (44, 48))
 HEAD_STEPS = 2
-SPLIT_STEP = 14
+SPLIT_STEP = 19
 
 
 def tile_coarsepyramid_pa_kernel(
@@ -50,7 +50,7 @@ def tile_coarsepyramid_pa_kernel(
         ps_bk = ctx.enter_context(tc.psum_pool(name="ps_bk", bufs=1))
         ps_st = ctx.enter_context(tc.psum_pool(name="ps_st", bufs=1))
         tabs = ctx.enter_context(tc.tile_pool(name="tabs", bufs=1))
-        fsp = ctx.enter_context(tc.tile_pool(name="fsp", bufs=4))
+        fsp = ctx.enter_context(tc.tile_pool(name="fsp", bufs=5))
         m2p = ctx.enter_context(tc.tile_pool(name="m2p", bufs=1))
         tsp = ctx.enter_context(tc.tile_pool(name="tsp", bufs=5))
         gp = ctx.enter_context(tc.tile_pool(name="gp", bufs=2 * (LAG + 1)))
@@ -65,7 +65,7 @@ def tile_coarsepyramid_pa_kernel(
         xscales = const.tile([P, NB * 64], U8, align_bytes=64)
         wcodes = const.tile([P, 1024], U32, align_bytes=64)
         wscales = const.tile([P, 1024], U8, align_bytes=64)
-        stats = const.tile([P, 8, 2 * NB, 3], F32)
+        stats = const.tile([P, 8, NB, 3], F32)
         gain = const.tile([P, 8, NB], F32)
         shift = const.tile([P, 8, NB], F32)
         idx = const.tile([P, 2, 48], I32)
@@ -73,11 +73,15 @@ def tile_coarsepyramid_pa_kernel(
         sc = const.tile([P, 4], F32)
         warm = const.tile([P, 2], F32)
         nc.gpsimd.memset(warm[:], 1.0)
+        side_i = const.tile([P, 48], I32)
+        nc.gpsimd.iota(side_i[:], pattern=[[0, 24], [1, 2]], base=0, channel_multiplier=0)
+        pidx = const.tile([P, 1], I32)
+        nc.gpsimd.iota(pidx[:], pattern=[[0, 1]], base=0, channel_multiplier=1)
 
         tbs = []
         for r in range(NTB):
             tb = tabs.tile([P, 8, NENT], F32, name="tb%d" % r)
-            nc.gpsimd.memset(tb[:], 0.0)
+            nc.gpsimd.memset(tb[:, :, ZERO0:NENT], 0.0)
             tbs.append(tb)
 
         rows = [o.rearrange("b (x y) n -> (b x) (y n)", y=8)[0:PARK_ROWS, :] for o in (out_1, out_0)]
@@ -104,12 +108,10 @@ def tile_coarsepyramid_pa_kernel(
             for s in range(2):
                 y = conv(i, s)
                 for u in range(4):
-                    for c in range(2):
-                        bp = 2 * i + c
-                        nc.vector.bn_stats(
-                            out=stats[:, 4 * s + u, 2 * bp:2 * bp + 2, :].rearrange("p i f -> p (i f)"),
-                            in_=y[:, u, c * 64:(c + 1) * 64],
-                        )
+                    nc.vector.bn_stats(
+                        out=stats[:, 4 * s + u, 2 * i:2 * i + 2, :].rearrange("p c f -> p (c f)"),
+                        in_=y[:, u, :].rearrange("p (c t) -> p t c", c=2),
+                    )
 
         def group_affine(p0, p1):
             b0, b1 = 2 * p0, 2 * p1
@@ -117,16 +119,16 @@ def tile_coarsepyramid_pa_kernel(
             bias_c = pv[:, 0, :, :, :]
             g_c = pv[:, 1, :, :, :]
             be_c = pv[:, 2, :, :, :]
-            mp = small.tile([P, 8, 2 * nb], F32, tag="mp")
+            mp = small.tile([P, 8, nb], F32, tag="mp")
             nc.vector.tensor_tensor(
-                out=mp[:], in0=stats[:, :, 2 * b0:2 * b1, 1],
-                in1=bias_c.rearrange("p s u o -> p (s u) o").to_broadcast([P, 8, 2 * nb]), op=ALU.add,
+                out=mp[:], in0=stats[:, :, b0:b1, 1],
+                in1=bias_c.rearrange("p s u o -> p (s u) o").to_broadcast([P, 8, nb]), op=ALU.add,
             )
-            sq = small.tile([P, 8, 2 * nb], F32, tag="sq")
+            sq = small.tile([P, 8, nb], F32, tag="sq")
             nc.vector.tensor_tensor(out=sq[:], in0=mp[:], in1=mp[:], op=ALU.mult)
-            v2 = small.tile([P, 8, 2 * nb], F32, tag="v2")
+            v2 = small.tile([P, 8, nb], F32, tag="v2")
             nc.vector.scalar_tensor_tensor(
-                out=v2[:], in0=stats[:, :, 2 * b0:2 * b1, 2], scalar=1.0 / 32.0, in1=sq[:],
+                out=v2[:], in0=stats[:, :, b0:b1, 2], scalar=1.0 / 64.0, in1=sq[:],
                 op0=ALU.mult, op1=ALU.add,
             )
             rs = small.tile([P, 2, 2, nb], F32, tag="rs")
@@ -134,8 +136,8 @@ def tile_coarsepyramid_pa_kernel(
                 for a, src in enumerate((mp, v2)):
                     nc.vector.tensor_reduce(
                         out=rs[:, a, s, :],
-                        in_=src[:, 4 * s:4 * s + 4, :].rearrange("p u (b i) -> p b u i", i=2),
-                        axis=AX.XY, op=ALU.add,
+                        in_=src[:, 4 * s:4 * s + 4, :].rearrange("p u b -> p b u"),
+                        axis=AX.X, op=ALU.add,
                     )
             pst = ps_st.tile([P, 4 * nb], F32, tag="pst")
             nc.tensor.matmul(
@@ -143,12 +145,12 @@ def tile_coarsepyramid_pa_kernel(
             )
             mu = small.tile([P, 2, 1, nb], F32, tag="mu")
             muf = mu[:].rearrange("p s o b -> p (s o b)")
-            nc.vector.tensor_scalar(out=muf, in0=pst[:, 0:2 * nb], scalar1=1.0 / 64.0, scalar2=None, op0=ALU.mult)
+            nc.vector.tensor_scalar(out=muf, in0=pst[:, 0:2 * nb], scalar1=1.0 / 32.0, scalar2=None, op0=ALU.mult)
             msq = small.tile([P, 2 * nb], F32, tag="msq")
             nc.vector.tensor_tensor(out=msq[:], in0=muf, in1=muf, op=ALU.mult)
             var = small.tile([P, 2 * nb], F32, tag="var")
             nc.vector.scalar_tensor_tensor(
-                out=var[:], in0=pst[:, 2 * nb:4 * nb], scalar=1.0 / 64.0, in1=msq[:], op0=ALU.mult, op1=ALU.subtract
+                out=var[:], in0=pst[:, 2 * nb:4 * nb], scalar=1.0 / 32.0, in1=msq[:], op0=ALU.mult, op1=ALU.subtract
             )
             nc.vector.tensor_scalar(out=var[:], in0=var[:], scalar1=EPS, scalar2=None, op0=ALU.add)
             sd = small.tile([P, 2 * nb], F32, tag="sd")
@@ -241,10 +243,10 @@ def tile_coarsepyramid_pa_kernel(
                 held0.append((i, fs))
             else:
                 fs = fsp.tile([P, 2, 8, 64], F32, tag="fs")
-                pending[1].append((i, fs))
             for c in range(2):
                 nc.scalar.copy(out=fs[:, c, :, :], in_=tb[:, :, c * 64:(c + 1) * 64])
-            flush(area)
+            if not late:
+                store_out0(i, fs)
             got = []
             for s in range(2):
                 col = 2 * ((i + ROT) % NPAIR) + s
@@ -273,9 +275,12 @@ def tile_coarsepyramid_pa_kernel(
                 bk = ps_bk.tile([P, 4, 128], F32, tag="bk")
                 for u in range(4):
                     nc.tensor.transpose(bk[:, u, :], ga[:, u * 128:(u + 1) * 128], ident[:])
-                nc.vector.tensor_copy(out=o1[:, :, s, :, :], in_=bk[:].rearrange("q u (c n) -> q c u n", c=2))
+                if s == 0:
+                    nc.scalar.copy(out=o1[:, :, s, :, :], in_=bk[:].rearrange("q u (c n) -> q c u n", c=2))
+                else:
+                    nc.vector.tensor_copy(out=o1[:, :, s, :, :], in_=bk[:].rearrange("q u (c n) -> q c u n", c=2))
             if not late:
-                pending[0].append((i, o1))
+                store_out1(i, o1)
 
         done = [0, 0, 0]
 
@@ -310,7 +315,7 @@ def tile_coarsepyramid_pa_kernel(
             front_a(i)
 
         def step(j, feat_chunk, after_tables):
-            ahead = min(NPAIR, 2 * j + 6)
+            ahead = min(NPAIR, j + 5)
             if j == 0:
                 activations(0, feat_chunk)
                 front_b(0, tbs[0], after_tables)
@@ -327,7 +332,7 @@ def tile_coarsepyramid_pa_kernel(
             late_stores(j)
             while done[0] < ahead:
                 stats_one(feat_chunk)
-            features_for(min(NPAIR, 2 * j + 8), feat_chunk)
+            features_for(min(NPAIR, j + 8), feat_chunk)
 
         with tc.tile_pool(name="prep", bufs=1) as prep, tc.tile_pool(name="prep2", bufs=2) as prep2:
             with tc.manual_schedule():
@@ -335,60 +340,26 @@ def tile_coarsepyramid_pa_kernel(
                 fv = feature_bytes.rearrange("b (p j) t -> j p b t", j=4)
                 w_sb = prep.tile([P, 2, 4, 512], BF16)
                 nc.sync.dma_start(out=sc[:], in_=feature_scale.rearrange("o (p j) i -> p (o j i)", j=4))
-                for li, (p0, p1) in enumerate(BYTE_LOADS):
-                    b0 = (p0 + 2 * ROT) % NB
-                    for j in range(4):
-                        nc.sync.dma_start(out=xb[:, j, p0:p1, :], in_=fv[j][:, b0:b0 + (p1 - p0), :])
-                    if li == 0:
-                        nc.sync.dma_start(
-                            out=w_sb[:].rearrange("q s u k -> q s (u k)"),
-                            in_=w_lr.rearrange("(s q u) k -> q s (u k)", s=2, u=4),
-                        )
-                pv_bf = prep.tile([P, 3, 16], BF16)
-                for m, vec in enumerate((b_lr, g_lr, be_lr)):
-                    nc.scalar.dma_start(
-                        out=pv_bf[:, m, 0:8].rearrange("q (s u) -> q s u", s=2),
-                        in_=vec.rearrange("(s q u) -> q s u", s=2, u=4),
-                    )
                 sg_bf = prep.tile([P, NPAIR, 4], BF16)
                 seg_v = segments.rearrange("(i c) n f -> c n i f", c=2)
                 for c in range(2):
-                    nc.scalar.dma_start(out=sg_bf[c * 64:(c + 1) * 64, :, :], in_=seg_v[c])
+                    nc.sync.dma_start(out=sg_bf[c * 64:(c + 1) * 64, :, :], in_=seg_v[c])
+                pv_bf = prep.tile([P, 3, 16], BF16)
+                for m, vec in enumerate((b_lr, g_lr, be_lr)):
+                    nc.sync.dma_start(
+                        out=pv_bf[:, m, 0:8].rearrange("q (s u) -> q s u", s=2),
+                        in_=vec.rearrange("(s q u) -> q s u", s=2, u=4),
+                    )
+                nc.sync.dma_start(
+                    out=w_sb[:].rearrange("q s u k -> q s (u k)"),
+                    in_=w_lr.rearrange("(s q u) k -> q s (u k)", s=2, u=4),
+                )
+                for p0, p1 in BYTE_LOADS:
+                    b0 = (p0 + 2 * ROT) % NB
+                    for j in range(4):
+                        nc.sync.dma_start(out=xb[:, j, p0:p1, :], in_=fv[j][:, b0:b0 + (p1 - p0), :])
                 nc.scalar.activation(out=warm[:, 1:2], in_=warm[:, 0:1], func=ACT.Sqrt)
                 nc.vector.tensor_copy(out=pv[:].rearrange("p m s u o -> p m (s u o)"), in_=pv_bf[:, :, 0:8])
-
-                def feat_chunk(p0, p1):
-                    n = p1 - p0
-                    gx = prep2.tile([P, n * 64, 4], BF16, tag="gx", align_bytes=64)
-                    for j in range(4):
-                        nc.vector.tensor_scalar(
-                            out=gx[:, :, j], in0=xb[:, j, p0:p1, :].rearrange("p b t -> p (b t)").bitcast(FP8),
-                            scalar1=sc[:, j:j + 1], scalar2=None, op0=ALU.mult,
-                        )
-                    nc.vector.quantize_mx(
-                        out=xcodes[:, p0 * 64:p1 * 64].bitcast(FP8X4),
-                        scales=xscales[:, p0 * 64:p1 * 64],
-                        in_=gx[:].rearrange("p c j -> p (c j)"),
-                    )
-
-                features_for(2, feat_chunk)
-
-                wg = prep.tile([P, 8, 128, 4], BF16, align_bytes=64)
-                for h in range(4):
-                    xt = ps_tp.tile([P, 2, 2, 128], F32, tag="tp")
-                    for a in range(2):
-                        tau = 2 * h + a
-                        words = w_sb[:, tau // 4, tau % 4, :].bitcast(F32)
-                        for v in range(2):
-                            nc.tensor.transpose(xt[:, a, v, :], words[:, v:256:2], ident[:])
-                    nc.vector.tensor_copy(
-                        out=wg[:, 2 * h:2 * h + 2, :, :].rearrange("p a q e -> p a (q e)").bitcast(F32)
-                        .rearrange("p a (q v) -> p a q v", v=2),
-                        in_=xt[:].rearrange("p a v q -> p a q v"),
-                    )
-                nc.vector.quantize_mx(
-                    out=wcodes[:].bitcast(FP8X4), scales=wscales[:], in_=wg[:].rearrange("p a q e -> p (a q e)")
-                )
 
                 def row_indices():
                     xs = prep.tile([P, 96], F32)
@@ -426,12 +397,8 @@ def tile_coarsepyramid_pa_kernel(
                     nc.vector.tensor_reduce(out=sa[:], in_=fa[:], axis=AX.X, op=ALU.add)
                     sd2 = prep.tile([P, 48], F32)
                     nc.vector.tensor_reduce(out=sd2[:], in_=fd[:], axis=AX.X, op=ALU.add)
-                    side_i = prep.tile([P, 48], I32)
-                    nc.gpsimd.iota(side_i[:], pattern=[[0, 24], [1, 2]], base=0, channel_multiplier=0)
                     side = prep.tile([P, 48], F32)
                     nc.vector.tensor_copy(out=side[:], in_=side_i[:])
-                    pidx = prep.tile([P, 1], I32)
-                    nc.gpsimd.iota(pidx[:], pattern=[[0, 1]], base=0, channel_multiplier=1)
                     pint = prep.tile([P, 2], I32)
                     nc.vector.tensor_single_scalar(out=pint[:, 0:1], in_=pidx[:], scalar=6, op=ALU.logical_shift_right)
                     nc.vector.tensor_single_scalar(out=pint[:, 1:2], in_=pidx[:], scalar=31, op=ALU.bitwise_and)
@@ -465,8 +432,43 @@ def tile_coarsepyramid_pa_kernel(
                         nc.vector.tensor_tensor(out=ri[:], in0=ri[:], in1=zidx[:], op=ALU.add)
                         nc.vector.tensor_copy(out=idx[:, e, :], in_=ri[:])
 
+                row_indices()
+
+                def feat_chunk(p0, p1):
+                    n = p1 - p0
+                    gx = prep2.tile([P, n * 64, 4], BF16, tag="gx", align_bytes=64)
+                    for j in range(4):
+                        nc.vector.tensor_scalar(
+                            out=gx[:, :, j], in0=xb[:, j, p0:p1, :].rearrange("p b t -> p (b t)").bitcast(FP8),
+                            scalar1=sc[:, j:j + 1], scalar2=None, op0=ALU.mult,
+                        )
+                    nc.vector.quantize_mx(
+                        out=xcodes[:, p0 * 64:p1 * 64].bitcast(FP8X4),
+                        scales=xscales[:, p0 * 64:p1 * 64],
+                        in_=gx[:].rearrange("p c j -> p (c j)"),
+                    )
+
+                features_for(2, feat_chunk)
+
+                wg = prep.tile([P, 8, 128, 4], BF16, align_bytes=64)
+                for h in range(4):
+                    xt = ps_tp.tile([P, 2, 2, 128], F32, tag="tp")
+                    for a in range(2):
+                        tau = 2 * h + a
+                        words = w_sb[:, tau // 4, tau % 4, :].bitcast(F32)
+                        for v in range(2):
+                            nc.tensor.transpose(xt[:, a, v, :], words[:, v:256:2], ident[:])
+                    nc.vector.tensor_copy(
+                        out=wg[:, 2 * h:2 * h + 2, :, :].rearrange("p a q e -> p a (q e)").bitcast(F32)
+                        .rearrange("p a (q v) -> p a q v", v=2),
+                        in_=xt[:].rearrange("p a v q -> p a q v"),
+                    )
+                nc.vector.quantize_mx(
+                    out=wcodes[:].bitcast(FP8X4), scales=wscales[:], in_=wg[:].rearrange("p a q e -> p (a q e)")
+                )
+
                 for j in range(HEAD_STEPS):
-                    step(j, feat_chunk, row_indices if j == 0 else None)
+                    step(j, feat_chunk, None)
             for j in range(HEAD_STEPS, SPLIT_STEP):
                 step(j, feat_chunk, None)
 

@@ -20,7 +20,8 @@ FLOPS = 2 * 48 * 1024 * 512 * 64
 P = 128
 NB = 48
 NPAIR = 24
-ROT = 5
+ORDER = (10, 11, 12, 13, 14, 15, 16, 17, 18, 19, 20, 21, 22, 23, 5, 6, 7, 8, 9, 0, 1, 2, 3, 4)
+NWIDE = 14
 NHOLD = 5
 PARK_ROWS = 1280
 WID = (1, 3, 6, 12, 24, 48)
@@ -32,7 +33,7 @@ EPS = 1e-5
 LAG = 3
 NTB = 2
 STAT_GROUPS = ((0, 1), (1, 3), (3, 6), (6, 9), (9, 12), (12, 15), (15, 18), (18, 21), (21, 24))
-BYTE_LOADS = ((0, 4), (4, 16), (16, 32), (32, 38), (38, 48))
+BYTE_LOADS = ((0, 4, 20), (4, 16, 24), (16, 28, 36), (28, 38, 10), (38, 48, 0))
 FEAT_CHUNKS = ((0, 2), (2, 4), (4, 8), (8, 12), (12, 16), (16, 20), (20, 24), (24, 28), (28, 32), (32, 36), (36, 40), (40, 44), (44, 48))
 HEAD_STEPS = 2
 SPLIT_STEP = 19
@@ -84,8 +85,12 @@ def tile_coarsepyramid_pa_kernel(
             nc.gpsimd.memset(tb[:, :, ZERO0:NENT], 0.0)
             tbs.append(tb)
 
-        rows = [o.rearrange("b (x y) n -> (b x) (y n)", y=8)[0:PARK_ROWS, :] for o in (out_1, out_0)]
-        parkv = [r.rearrange("(r p s) e -> p r (s e)", p=P, s=2) for r in rows]
+        allrows = [o.rearrange("b (x y) n -> (b x) (y n)", y=8) for o in (out_1, out_0)]
+        rows = [[r[0:PARK_ROWS, :], r[0:2 * PARK_ROWS, :]] for r in allrows]
+        parkv = [
+            [r[h * PARK_ROWS:(h + 1) * PARK_ROWS, :].rearrange("(r p s) e -> p r (s e)", p=P, s=2) for h in range(2)]
+            for r in allrows
+        ]
         o0v = out_0.rearrange("b (s q u) t -> q (b s) (u t)", s=2, u=4)
         o1v = out_1.rearrange("b (s q u) n -> q (b s) (u n)", s=2, u=4)
 
@@ -169,13 +174,13 @@ def tile_coarsepyramid_pa_kernel(
             nc.vector.tensor_tensor(out=sh, in0=t1[:], in1=be_c.to_broadcast(full), op=ALU.add)
 
         def store_out0(i, fs):
-            b0 = (2 * (i + ROT)) % NB
+            b0 = 2 * ORDER[i]
             nc.sync.dma_start(
                 out=o0v[:, 2 * b0:2 * b0 + 4, :], in_=fs[:].rearrange("q c (s u) t -> q (c s) (u t)", s=2)
             )
 
         def store_out1(i, o1):
-            b0 = (2 * (i + ROT)) % NB
+            b0 = 2 * ORDER[i]
             nc.sync.dma_start(out=o1v[:, 2 * b0:2 * b0 + 4, :], in_=o1[:].rearrange("q c s u n -> q (c s) (u n)"))
 
         pending = [[], []]
@@ -224,6 +229,7 @@ def tile_coarsepyramid_pa_kernel(
             if after_tables is not None:
                 after_tables()
             area = i % 2
+            upper = (i // 2) % 2 if i < NWIDE else 0
             for g in range(3):
                 nr = min(2, 5 - 2 * g)
                 tsb = tsp.tile([P, 2, 2, 512], F32, tag="tsb")
@@ -235,7 +241,8 @@ def tile_coarsepyramid_pa_kernel(
                             nc.tensor.transpose(tp[:, u, :], tb[:, 4 * s + u, r * 128:(r + 1) * 128], ident[:])
                         nc.scalar.copy(out=tsb[:, rl, s, :], in_=tp[:].rearrange("p u q -> p (u q)"))
                 nc.sync.dma_start(
-                    out=parkv[area][:, 2 * g:2 * g + nr, :], in_=tsb[:, 0:nr, :, :].rearrange("p r s e -> p r (s e)")
+                    out=parkv[area][upper][:, 2 * g:2 * g + nr, :],
+                    in_=tsb[:, 0:nr, :, :].rearrange("p r s e -> p r (s e)"),
                 )
             late = i >= NPAIR - NHOLD
             if late:
@@ -249,12 +256,12 @@ def tile_coarsepyramid_pa_kernel(
                 store_out0(i, fs)
             got = []
             for s in range(2):
-                col = 2 * ((i + ROT) % NPAIR) + s
+                col = 2 * ORDER[i] + s
                 pairg = []
                 for e in range(2):
                     g = gp.tile([P, 512], F32, tag="g%d" % e)
                     nc.gpsimd.indirect_dma_start(
-                        out=g[:], out_offset=None, in_=rows[area],
+                        out=g[:], out_offset=None, in_=rows[area][upper],
                         in_offset=bass.IndirectOffsetOnAxis(ap=idx[:, e, col:col + 1], axis=0),
                     )
                     pairg.append(g)
@@ -354,8 +361,7 @@ def tile_coarsepyramid_pa_kernel(
                     out=w_sb[:].rearrange("q s u k -> q s (u k)"),
                     in_=w_lr.rearrange("(s q u) k -> q s (u k)", s=2, u=4),
                 )
-                for p0, p1 in BYTE_LOADS:
-                    b0 = (p0 + 2 * ROT) % NB
+                for p0, p1, b0 in BYTE_LOADS:
                     for j in range(4):
                         nc.sync.dma_start(out=xb[:, j, p0:p1, :], in_=fv[j][:, b0:b0 + (p1 - p0), :])
                 nc.scalar.activation(out=warm[:, 1:2], in_=warm[:, 0:1], func=ACT.Sqrt)
@@ -418,6 +424,13 @@ def tile_coarsepyramid_pa_kernel(
                     nc.vector.tensor_tensor(out=com[:], in0=sa[:], in1=cd[:], op=ALU.subtract)
                     nc.vector.tensor_tensor(out=com[:], in0=com[:], in1=side[:], op=ALU.add)
                     nc.vector.tensor_scalar(out=com[:], in0=com[:], scalar1=c128[:, 0:1], scalar2=None, op0=ALU.add)
+                    ofs = prep.tile([P, 48], F32)
+                    nc.vector.memset(ofs[:], 0.0)
+                    for i in range(NWIDE):
+                        if (i // 2) % 2 == 1:
+                            nc.vector.memset(ofs[:, 2 * ORDER[i]:2 * ORDER[i] + 2], float(PARK_ROWS))
+                    nc.vector.tensor_tensor(out=zidx[:], in0=zidx[:], in1=ofs[:], op=ALU.add)
+                    nc.vector.tensor_tensor(out=com[:], in0=com[:], in1=ofs[:], op=ALU.add)
                     for e, (pos, thr) in enumerate(((lo, 0.0), (hi, 1.0))):
                         ri = prep.tile([P, 48], F32, name="ri%d" % e)
                         nc.vector.scalar_tensor_tensor(

@@ -20,8 +20,7 @@ FLOPS = 2 * 48 * 1024 * 512 * 64
 P = 128
 NB = 48
 NPAIR = 24
-ORDER = (10, 11, 12, 13, 14, 15, 16, 17, 18, 19, 20, 21, 22, 23, 5, 6, 7, 8, 9, 0, 1, 2, 3, 4)
-NWIDE = 14
+ROT = 5
 NHOLD = 5
 PARK_ROWS = 1280
 WID = (1, 3, 6, 12, 24, 48)
@@ -33,7 +32,7 @@ EPS = 1e-5
 LAG = 3
 NTB = 2
 STAT_GROUPS = ((0, 1), (1, 3), (3, 6), (6, 9), (9, 12), (12, 15), (15, 18), (18, 21), (21, 24))
-BYTE_LOADS = ((0, 4, 20), (4, 16, 24), (16, 28, 36), (28, 38, 10), (38, 48, 0))
+BYTE_LOADS = ((0, 4), (4, 16), (16, 32), (32, 38), (38, 48))
 FEAT_CHUNKS = ((0, 2), (2, 4), (4, 8), (8, 12), (12, 16), (16, 20), (20, 24), (24, 28), (28, 32), (32, 36), (36, 40), (40, 44), (44, 48))
 HEAD_STEPS = 2
 SPLIT_STEP = 19
@@ -46,7 +45,7 @@ def tile_coarsepyramid_pa_kernel(
     with ExitStack() as ctx:
         const = ctx.enter_context(tc.tile_pool(name="const", bufs=1))
         small = ctx.enter_context(tc.tile_pool(name="small", bufs=2))
-        ps_y = ctx.enter_context(tc.psum_pool(name="ps_y", bufs=3))
+        ps_y = ctx.enter_context(tc.psum_pool(name="ps_y", bufs=2))
         ps_tp = ctx.enter_context(tc.psum_pool(name="ps_tp", bufs=3))
         ps_bk = ctx.enter_context(tc.psum_pool(name="ps_bk", bufs=1))
         ps_st = ctx.enter_context(tc.psum_pool(name="ps_st", bufs=1))
@@ -56,6 +55,7 @@ def tile_coarsepyramid_pa_kernel(
         tsp = ctx.enter_context(tc.tile_pool(name="tsp", bufs=5))
         gp = ctx.enter_context(tc.tile_pool(name="gp", bufs=2 * (LAG + 1)))
         o1p = ctx.enter_context(tc.tile_pool(name="o1p", bufs=4))
+        etp = ctx.enter_context(tc.tile_pool(name="etp", bufs=2))
 
         ident = const.tile([P, P], F32)
         make_identity(nc, ident[:])
@@ -85,12 +85,8 @@ def tile_coarsepyramid_pa_kernel(
             nc.gpsimd.memset(tb[:, :, ZERO0:NENT], 0.0)
             tbs.append(tb)
 
-        allrows = [o.rearrange("b (x y) n -> (b x) (y n)", y=8) for o in (out_1, out_0)]
-        rows = [[r[0:PARK_ROWS, :], r[0:2 * PARK_ROWS, :]] for r in allrows]
-        parkv = [
-            [r[h * PARK_ROWS:(h + 1) * PARK_ROWS, :].rearrange("(r p s) e -> p r (s e)", p=P, s=2) for h in range(2)]
-            for r in allrows
-        ]
+        rows = [o.rearrange("b (x y) n -> (b x) (y n)", y=8)[0:PARK_ROWS, :] for o in (out_1, out_0)]
+        parkv = [r.rearrange("(r p s) e -> p r (s e)", p=P, s=2) for r in rows]
         o0v = out_0.rearrange("b (s q u) t -> q (b s) (u t)", s=2, u=4)
         o1v = out_1.rearrange("b (s q u) n -> q (b s) (u n)", s=2, u=4)
 
@@ -174,13 +170,13 @@ def tile_coarsepyramid_pa_kernel(
             nc.vector.tensor_tensor(out=sh, in0=t1[:], in1=be_c.to_broadcast(full), op=ALU.add)
 
         def store_out0(i, fs):
-            b0 = 2 * ORDER[i]
+            b0 = (2 * (i + ROT)) % NB
             nc.sync.dma_start(
                 out=o0v[:, 2 * b0:2 * b0 + 4, :], in_=fs[:].rearrange("q c (s u) t -> q (c s) (u t)", s=2)
             )
 
         def store_out1(i, o1):
-            b0 = 2 * ORDER[i]
+            b0 = (2 * (i + ROT)) % NB
             nc.sync.dma_start(out=o1v[:, 2 * b0:2 * b0 + 4, :], in_=o1[:].rearrange("q c s u n -> q (c s) (u n)"))
 
         pending = [[], []]
@@ -229,7 +225,6 @@ def tile_coarsepyramid_pa_kernel(
             if after_tables is not None:
                 after_tables()
             area = i % 2
-            upper = (i // 2) % 2 if i < NWIDE else 0
             for g in range(3):
                 nr = min(2, 5 - 2 * g)
                 tsb = tsp.tile([P, 2, 2, 512], F32, tag="tsb")
@@ -241,8 +236,7 @@ def tile_coarsepyramid_pa_kernel(
                             nc.tensor.transpose(tp[:, u, :], tb[:, 4 * s + u, r * 128:(r + 1) * 128], ident[:])
                         nc.scalar.copy(out=tsb[:, rl, s, :], in_=tp[:].rearrange("p u q -> p (u q)"))
                 nc.sync.dma_start(
-                    out=parkv[area][upper][:, 2 * g:2 * g + nr, :],
-                    in_=tsb[:, 0:nr, :, :].rearrange("p r s e -> p r (s e)"),
+                    out=parkv[area][:, 2 * g:2 * g + nr, :], in_=tsb[:, 0:nr, :, :].rearrange("p r s e -> p r (s e)")
                 )
             late = i >= NPAIR - NHOLD
             if late:
@@ -256,12 +250,12 @@ def tile_coarsepyramid_pa_kernel(
                 store_out0(i, fs)
             got = []
             for s in range(2):
-                col = 2 * ORDER[i] + s
+                col = 2 * ((i + ROT) % NPAIR) + s
                 pairg = []
                 for e in range(2):
                     g = gp.tile([P, 512], F32, tag="g%d" % e)
                     nc.gpsimd.indirect_dma_start(
-                        out=g[:], out_offset=None, in_=rows[area][upper],
+                        out=g[:], out_offset=None, in_=rows[area],
                         in_offset=bass.IndirectOffsetOnAxis(ap=idx[:, e, col:col + 1], axis=0),
                     )
                     pairg.append(g)
@@ -276,16 +270,18 @@ def tile_coarsepyramid_pa_kernel(
                 o1 = o1p.tile([P, 2, 2, 4, 64], F32, tag="o1")
             for s in range(2):
                 ga, ge = gathered[i][s]
-                nc.vector.tensor_tensor(out=ga[:], in0=ga[:], in1=ge[:], op=ALU.max)
-            for s in range(2):
-                ga, ge = gathered[i][s]
-                bk = ps_bk.tile([P, 4, 128], F32, tag="bk")
+                bkb = ps_bk.tile([P, 4, 128], F32, tag="bkb")
                 for u in range(4):
-                    nc.tensor.transpose(bk[:, u, :], ga[:, u * 128:(u + 1) * 128], ident[:])
-                if s == 0:
-                    nc.scalar.copy(out=o1[:, :, s, :, :], in_=bk[:].rearrange("q u (c n) -> q c u n", c=2))
-                else:
-                    nc.vector.tensor_copy(out=o1[:, :, s, :, :], in_=bk[:].rearrange("q u (c n) -> q c u n", c=2))
+                    nc.tensor.transpose(bkb[:, u, :], ge[:, u * 128:(u + 1) * 128], ident[:])
+                bka = ps_bk.tile([P, 4, 128], F32, tag="bka")
+                for u in range(4):
+                    nc.tensor.transpose(bka[:, u, :], ga[:, u * 128:(u + 1) * 128], ident[:])
+                et = etp.tile([P, 4, 128], F32, tag="et")
+                nc.scalar.copy(out=et[:], in_=bkb[:])
+                nc.vector.tensor_tensor(
+                    out=o1[:, :, s, :, :], in0=bka[:].rearrange("q u (c n) -> q c u n", c=2),
+                    in1=et[:].rearrange("q u (c n) -> q c u n", c=2), op=ALU.max,
+                )
             if not late:
                 store_out1(i, o1)
 
@@ -361,7 +357,8 @@ def tile_coarsepyramid_pa_kernel(
                     out=w_sb[:].rearrange("q s u k -> q s (u k)"),
                     in_=w_lr.rearrange("(s q u) k -> q s (u k)", s=2, u=4),
                 )
-                for p0, p1, b0 in BYTE_LOADS:
+                for p0, p1 in BYTE_LOADS:
+                    b0 = (p0 + 2 * ROT) % NB
                     for j in range(4):
                         nc.sync.dma_start(out=xb[:, j, p0:p1, :], in_=fv[j][:, b0:b0 + (p1 - p0), :])
                 nc.scalar.activation(out=warm[:, 1:2], in_=warm[:, 0:1], func=ACT.Sqrt)
@@ -424,13 +421,6 @@ def tile_coarsepyramid_pa_kernel(
                     nc.vector.tensor_tensor(out=com[:], in0=sa[:], in1=cd[:], op=ALU.subtract)
                     nc.vector.tensor_tensor(out=com[:], in0=com[:], in1=side[:], op=ALU.add)
                     nc.vector.tensor_scalar(out=com[:], in0=com[:], scalar1=c128[:, 0:1], scalar2=None, op0=ALU.add)
-                    ofs = prep.tile([P, 48], F32)
-                    nc.vector.memset(ofs[:], 0.0)
-                    for i in range(NWIDE):
-                        if (i // 2) % 2 == 1:
-                            nc.vector.memset(ofs[:, 2 * ORDER[i]:2 * ORDER[i] + 2], float(PARK_ROWS))
-                    nc.vector.tensor_tensor(out=zidx[:], in0=zidx[:], in1=ofs[:], op=ALU.add)
-                    nc.vector.tensor_tensor(out=com[:], in0=com[:], in1=ofs[:], op=ALU.add)
                     for e, (pos, thr) in enumerate(((lo, 0.0), (hi, 1.0))):
                         ri = prep.tile([P, 48], F32, name="ri%d" % e)
                         nc.vector.scalar_tensor_tensor(

@@ -86,7 +86,7 @@ def tile_coarsepyramid_pa_kernel(
             tbs.append(tb)
 
         rows = [o.rearrange("b (x y) n -> (b x) (y n)", y=8)[0:PARK_ROWS, :] for o in (out_1, out_0)]
-        parkv = [r.rearrange("(r p s) e -> p r (s e)", p=P, s=2) for r in rows]
+        parkv = [r.rearrange("(p r s) e -> p r (s e)", p=P, s=2) for r in rows]
         o0v = out_0.rearrange("b (s q u) t -> q (b s) (u t)", s=2, u=4)
         o1v = out_1.rearrange("b (s q u) n -> q (b s) (u n)", s=2, u=4)
 
@@ -153,9 +153,8 @@ def tile_coarsepyramid_pa_kernel(
             nc.vector.scalar_tensor_tensor(
                 out=var[:], in0=pst[:, 2 * nb:4 * nb], scalar=1.0 / 32.0, in1=msq[:], op0=ALU.mult, op1=ALU.subtract
             )
-            nc.vector.tensor_scalar(out=var[:], in0=var[:], scalar1=EPS, scalar2=None, op0=ALU.add)
             sd = small.tile([P, 2 * nb], F32, tag="sd")
-            nc.scalar.activation(out=sd[:], in_=var[:], func=ACT.Sqrt)
+            nc.scalar.activation(out=sd[:], in_=var[:], func=ACT.Sqrt, bias=EPS)
             rstd = small.tile([P, 2, 1, nb], F32, tag="rstd")
             nc.vector.reciprocal(out=rstd[:].rearrange("p s o b -> p (s o b)"), in_=sd[:])
             full = [P, 2, 4, nb]
@@ -235,8 +234,10 @@ def tile_coarsepyramid_pa_kernel(
                         for u in range(4):
                             nc.tensor.transpose(tp[:, u, :], tb[:, 4 * s + u, r * 128:(r + 1) * 128], ident[:])
                         nc.scalar.copy(out=tsb[:, rl, s, :], in_=tp[:].rearrange("p u q -> p (u q)"))
+                nump = P if (g < 2 or i < 2) else ZERO0 - 512
                 nc.sync.dma_start(
-                    out=parkv[area][:, 2 * g:2 * g + nr, :], in_=tsb[:, 0:nr, :, :].rearrange("p r s e -> p r (s e)")
+                    out=parkv[area][0:nump, 2 * g:2 * g + nr, :],
+                    in_=tsb[0:nump, 0:nr, :, :].rearrange("p r s e -> p r (s e)"),
                 )
             late = i >= NPAIR - NHOLD
             if late:
@@ -434,6 +435,23 @@ def tile_coarsepyramid_pa_kernel(
                         nc.vector.tensor_tensor(out=ri[:], in0=ri[:], in1=ne[:], op=ALU.mult)
                         nc.vector.tensor_tensor(out=ri[:], in0=ri[:], in1=zidx[:], op=ALU.add)
                         nc.vector.tensor_copy(out=idx[:, e, :], in_=ri[:])
+                    part = prep.tile([P, 3, 96], I32)
+                    idf = idx[:].rearrange("p e c -> p (e c)")
+                    nc.vector.tensor_single_scalar(out=part[:, 0, :], in_=idf, scalar=8, op=ALU.logical_shift_right)
+                    nc.vector.tensor_scalar(
+                        out=part[:, 1, :], in0=idf, scalar1=1, scalar2=127,
+                        op0=ALU.logical_shift_right, op1=ALU.bitwise_and,
+                    )
+                    nc.vector.tensor_single_scalar(out=part[:, 2, :], in_=idf, scalar=1, op=ALU.bitwise_and)
+                    partf = prep.tile([P, 3, 96], F32)
+                    nc.vector.tensor_copy(out=partf[:], in_=part[:])
+                    nc.vector.scalar_tensor_tensor(
+                        out=partf[:, 2, :], in0=partf[:, 1, :], scalar=10.0, in1=partf[:, 2, :], op0=ALU.mult, op1=ALU.add
+                    )
+                    nc.vector.scalar_tensor_tensor(
+                        out=partf[:, 2, :], in0=partf[:, 0, :], scalar=2.0, in1=partf[:, 2, :], op0=ALU.mult, op1=ALU.add
+                    )
+                    nc.vector.tensor_copy(out=idf, in_=partf[:, 2, :])
 
                 row_indices()
 

@@ -47,7 +47,7 @@ def tile_coarsepyramid_pa_kernel(
         small = ctx.enter_context(tc.tile_pool(name="small", bufs=2))
         ps_y = ctx.enter_context(tc.psum_pool(name="ps_y", bufs=2))
         ps_tp = ctx.enter_context(tc.psum_pool(name="ps_tp", bufs=3))
-        ps_bk = ctx.enter_context(tc.psum_pool(name="ps_bk", bufs=1))
+        ps_bk = ctx.enter_context(tc.psum_pool(name="ps_bk", bufs=2))
         ps_st = ctx.enter_context(tc.psum_pool(name="ps_st", bufs=1))
         tabs = ctx.enter_context(tc.tile_pool(name="tabs", bufs=1))
         fsp = ctx.enter_context(tc.tile_pool(name="fsp", bufs=5))
@@ -55,7 +55,6 @@ def tile_coarsepyramid_pa_kernel(
         tsp = ctx.enter_context(tc.tile_pool(name="tsp", bufs=5))
         gp = ctx.enter_context(tc.tile_pool(name="gp", bufs=2 * (LAG + 1)))
         o1p = ctx.enter_context(tc.tile_pool(name="o1p", bufs=4))
-        etp = ctx.enter_context(tc.tile_pool(name="etp", bufs=2))
 
         ident = const.tile([P, P], F32)
         make_identity(nc, ident[:])
@@ -271,18 +270,17 @@ def tile_coarsepyramid_pa_kernel(
                 o1 = o1p.tile([P, 2, 2, 4, 64], F32, tag="o1")
             for s in range(2):
                 ga, ge = gathered[i][s]
-                bkb = ps_bk.tile([P, 4, 128], F32, tag="bkb")
-                for u in range(4):
-                    nc.tensor.transpose(bkb[:, u, :], ge[:, u * 128:(u + 1) * 128], ident[:])
-                bka = ps_bk.tile([P, 4, 128], F32, tag="bka")
-                for u in range(4):
-                    nc.tensor.transpose(bka[:, u, :], ga[:, u * 128:(u + 1) * 128], ident[:])
-                et = etp.tile([P, 4, 128], F32, tag="et")
-                nc.scalar.copy(out=et[:], in_=bkb[:])
-                nc.vector.tensor_tensor(
-                    out=o1[:, :, s, :, :], in0=bka[:].rearrange("q u (c n) -> q c u n", c=2),
-                    in1=et[:].rearrange("q u (c n) -> q c u n", c=2), op=ALU.max,
-                )
+                for h in range(2):
+                    bk = ps_bk.tile([P, 2, 2, 128], F32, tag="bk")
+                    for ul in range(2):
+                        u = 2 * h + ul
+                        for e, g in enumerate((ga, ge)):
+                            nc.tensor.transpose(bk[:, e, ul, :], g[:, u * 128:(u + 1) * 128], ident[:])
+                    nc.vector.tensor_reduce(
+                        out=o1[:, :, s, 2 * h:2 * h + 2, :].rearrange("q c u n -> q u c n"),
+                        in_=bk[:].rearrange("q e u (c n) -> q u c n e", c=2),
+                        axis=AX.X, op=ALU.max,
+                    )
             if not late:
                 store_out1(i, o1)
 

@@ -20,7 +20,7 @@ FLOPS = 2 * 48 * 1024 * 512 * 64
 P = 128
 NB = 48
 NPAIR = 24
-ROT = 5
+NFOUR = 14
 NHOLD = 5
 PARK_ROWS = 1280
 WID = (1, 3, 6, 12, 24, 48)
@@ -32,7 +32,7 @@ EPS = 1e-5
 LAG = 3
 NTB = 2
 STAT_GROUPS = ((0, 1), (1, 3), (3, 6), (6, 9), (9, 12), (12, 15), (15, 18), (18, 21), (21, 24))
-BYTE_LOADS = ((0, 4), (4, 16), (16, 32), (32, 38), (38, 48))
+BYTE_LOADS = ((0, 4), (4, 16), (16, 28), (28, 38), (38, 48))
 FEAT_CHUNKS = ((0, 2), (2, 4), (4, 8), (8, 12), (12, 16), (16, 20), (20, 24), (24, 28), (28, 32), (32, 36), (36, 40), (40, 44), (44, 48))
 HEAD_STEPS = 2
 SPLIT_STEP = 19
@@ -55,6 +55,7 @@ def tile_coarsepyramid_pa_kernel(
         tsp = ctx.enter_context(tc.tile_pool(name="tsp", bufs=5))
         gp = ctx.enter_context(tc.tile_pool(name="gp", bufs=2 * (LAG + 1)))
         o1p = ctx.enter_context(tc.tile_pool(name="o1p", bufs=4))
+        etp = ctx.enter_context(tc.tile_pool(name="etp", bufs=2))
 
         ident = const.tile([P, P], F32)
         make_identity(nc, ident[:])
@@ -84,8 +85,19 @@ def tile_coarsepyramid_pa_kernel(
             nc.gpsimd.memset(tb[:, :, ZERO0:NENT], 0.0)
             tbs.append(tb)
 
-        rows = [o.rearrange("b (x y) n -> (b x) (y n)", y=8)[0:PARK_ROWS, :] for o in (out_1, out_0)]
-        parkv = [r.rearrange("(p r s) e -> p r (s e)", p=P, s=2) for r in rows]
+        flat = [o.rearrange("b (x y) n -> (b x) (y n)", y=8) for o in (out_1, out_0)]
+        rows = [flat[k % 2][0:(1 + k // 2) * PARK_ROWS, :] for k in range(4)]
+        spots = [flat[k % 2][(k // 2) * PARK_ROWS:(1 + k // 2) * PARK_ROWS, :] for k in range(4)]
+
+        def which(i):
+            if i < NFOUR:
+                return i + 10
+            return i - 9 if i < NPAIR - NHOLD else i - (NPAIR - NHOLD)
+
+        def place(i):
+            return i % 4 if i < NFOUR else i % 2
+
+        parkv = [r.rearrange("(p r s) e -> p r (s e)", p=P, s=2) for r in spots]
         o0v = out_0.rearrange("b (s q u) t -> q (b s) (u t)", s=2, u=4)
         o1v = out_1.rearrange("b (s q u) n -> q (b s) (u n)", s=2, u=4)
 
@@ -168,13 +180,13 @@ def tile_coarsepyramid_pa_kernel(
             nc.vector.tensor_tensor(out=sh, in0=t1[:], in1=be_c.to_broadcast(full), op=ALU.add)
 
         def store_out0(i, fs):
-            b0 = (2 * (i + ROT)) % NB
+            b0 = 2 * which(i)
             nc.sync.dma_start(
                 out=o0v[:, 2 * b0:2 * b0 + 4, :], in_=fs[:].rearrange("q c (s u) t -> q (c s) (u t)", s=2)
             )
 
         def store_out1(i, o1):
-            b0 = (2 * (i + ROT)) % NB
+            b0 = 2 * which(i)
             nc.sync.dma_start(out=o1v[:, 2 * b0:2 * b0 + 4, :], in_=o1[:].rearrange("q c s u n -> q (c s) (u n)"))
 
         pending = [[], []]
@@ -222,7 +234,7 @@ def tile_coarsepyramid_pa_kernel(
                 )
             if after_tables is not None:
                 after_tables()
-            area = i % 2
+            area = place(i)
             for g in range(3):
                 nr = min(2, 5 - 2 * g)
                 tsb = tsp.tile([P, 2, 2, 512], F32, tag="tsb")
@@ -233,7 +245,7 @@ def tile_coarsepyramid_pa_kernel(
                         for u in range(4):
                             nc.tensor.transpose(tp[:, u, :], tb[:, 4 * s + u, r * 128:(r + 1) * 128], ident[:])
                         nc.scalar.copy(out=tsb[:, rl, s, :], in_=tp[:].rearrange("p u q -> p (u q)"))
-                nump = P if (g < 2 or i < 2) else ZERO0 - 512
+                nump = P if (g < 2 or i < 4) else ZERO0 - 512
                 nc.sync.dma_start(
                     out=parkv[area][0:nump, 2 * g:2 * g + nr, :],
                     in_=tsb[0:nump, 0:nr, :, :].rearrange("p r s e -> p r (s e)"),
@@ -250,7 +262,7 @@ def tile_coarsepyramid_pa_kernel(
                 store_out0(i, fs)
             got = []
             for s in range(2):
-                col = 2 * ((i + ROT) % NPAIR) + s
+                col = 2 * which(i) + s
                 pairg = []
                 for e in range(2):
                     g = gp.tile([P, 512], F32, tag="g%d" % e)
@@ -270,7 +282,20 @@ def tile_coarsepyramid_pa_kernel(
                 o1 = o1p.tile([P, 2, 2, 4, 64], F32, tag="o1")
             for s in range(2):
                 ga, ge = gathered[i][s]
-                for h in range(2):
+                if s == 1:
+                    bkb = ps_bk.tile([P, 4, 128], F32, tag="bk")
+                    for u in range(4):
+                        nc.tensor.transpose(bkb[:, u, :], ge[:, u * 128:(u + 1) * 128], ident[:])
+                    bka = ps_bk.tile([P, 4, 128], F32, tag="bk")
+                    for u in range(4):
+                        nc.tensor.transpose(bka[:, u, :], ga[:, u * 128:(u + 1) * 128], ident[:])
+                    et = etp.tile([P, 4, 128], F32, tag="et")
+                    nc.scalar.copy(out=et[:], in_=bkb[:])
+                    nc.vector.tensor_tensor(
+                        out=o1[:, :, s, :, :], in0=bka[:].rearrange("q u (c n) -> q c u n", c=2),
+                        in1=et[:].rearrange("q u (c n) -> q c u n", c=2), op=ALU.max,
+                    )
+                for h in range(2 - 2 * s):
                     bk = ps_bk.tile([P, 2, 2, 128], F32, tag="bk")
                     for ul in range(2):
                         u = 2 * h + ul
@@ -357,7 +382,7 @@ def tile_coarsepyramid_pa_kernel(
                     in_=w_lr.rearrange("(s q u) k -> q s (u k)", s=2, u=4),
                 )
                 for p0, p1 in BYTE_LOADS:
-                    b0 = (p0 + 2 * ROT) % NB
+                    b0 = 2 * which(p0 // 2)
                     for j in range(4):
                         nc.sync.dma_start(out=xb[:, j, p0:p1, :], in_=fv[j][:, b0:b0 + (p1 - p0), :])
                 nc.scalar.activation(out=warm[:, 1:2], in_=warm[:, 0:1], func=ACT.Sqrt)
@@ -449,6 +474,13 @@ def tile_coarsepyramid_pa_kernel(
                     nc.vector.scalar_tensor_tensor(
                         out=partf[:, 2, :], in0=partf[:, 0, :], scalar=2.0, in1=partf[:, 2, :], op0=ALU.mult, op1=ALU.add
                     )
+                    for i in range(NFOUR):
+                        if place(i) >= 2 and place(i) % 2 == 0:
+                            c0 = 2 * which(i)
+                            upper = partf[:, 2, :].rearrange("p (e c) -> p e c", e=2)[:, :, c0:c0 + 4]
+                            nc.vector.tensor_scalar(
+                                out=upper, in0=upper, scalar1=float(PARK_ROWS), scalar2=None, op0=ALU.add
+                            )
                     nc.vector.tensor_copy(out=idf, in_=partf[:, 2, :])
 
                 row_indices()

@@ -35,7 +35,9 @@ STAT_GROUPS = ((0, 1), (1, 3), (3, 6), (6, 9), (9, 12), (12, 15), (15, 18), (18,
 BYTE_LOADS = ((0, 4), (4, 16), (16, 28), (28, 38), (38, 48))
 FEAT_CHUNKS = ((0, 2), (2, 4), (4, 8), (8, 12), (12, 16), (16, 20), (20, 24), (24, 28), (28, 32), (32, 36), (36, 40), (40, 44), (44, 48))
 HEAD_STEPS = 2
-SPLIT_STEP = 19
+S_CHUNKS = 4
+S_BATCHES = 32
+SPLIT_STEP = 18
 
 
 def tile_coarsepyramid_pa_kernel(
@@ -52,7 +54,8 @@ def tile_coarsepyramid_pa_kernel(
         tabs = ctx.enter_context(tc.tile_pool(name="tabs", bufs=1))
         fsp = ctx.enter_context(tc.tile_pool(name="fsp", bufs=5))
         m2p = ctx.enter_context(tc.tile_pool(name="m2p", bufs=1))
-        tsp = ctx.enter_context(tc.tile_pool(name="tsp", bufs=5))
+        tsp = ctx.enter_context(tc.tile_pool(name="tsp", bufs=4))
+        tsp0 = ctx.enter_context(tc.tile_pool(name="tsp0", bufs=3))
         gp = ctx.enter_context(tc.tile_pool(name="gp", bufs=2 * (LAG + 1)))
         o1p = ctx.enter_context(tc.tile_pool(name="o1p", bufs=4))
         etp = ctx.enter_context(tc.tile_pool(name="etp", bufs=2))
@@ -81,8 +84,8 @@ def tile_coarsepyramid_pa_kernel(
 
         tbs = []
         for r in range(NTB):
-            tb = tabs.tile([P, 8, NENT], F32, name="tb%d" % r)
-            nc.gpsimd.memset(tb[:, :, ZERO0:NENT], 0.0)
+            tb = tabs.tile([P, 8, NENT - 128], F32, name="tb%d" % r)
+            nc.gpsimd.memset(tb[:, :, ZERO0 - 128:NENT - 128], 0.0)
             tbs.append(tb)
 
         flat = [o.rearrange("b (x y) n -> (b x) (y n)", y=8) for o in (out_1, out_0)]
@@ -98,6 +101,7 @@ def tile_coarsepyramid_pa_kernel(
             return i % 4 if i < NFOUR else i % 2
 
         parkv = [r.rearrange("(p r s) e -> p r (s e)", p=P, s=2) for r in spots]
+        park0 = [pk[:, 0, :].rearrange("p (k v q) -> v p k q", k=4, v=2) for pk in parkv]
         o0v = out_0.rearrange("b (s q u) t -> q (b s) (u t)", s=2, u=4)
         o1v = out_1.rearrange("b (s q u) n -> q (b s) (u n)", s=2, u=4)
 
@@ -204,8 +208,15 @@ def tile_coarsepyramid_pa_kernel(
         gathered = {}
         pools = {}
 
+        feats = {}
+
         def front_a(i):
-            tb = tbs[i % NTB]
+            if i >= NPAIR - NHOLD:
+                fs = pools["hold"].tile([P, 2, 8, 64], F32, name="fsh%d" % i)
+                held0.append((i, fs))
+            else:
+                fs = fsp.tile([P, 2, 8, 64], F32, tag="fs")
+            feats[i] = fs
             for s in range(2):
                 y = conv(i, s)
                 for u in range(4):
@@ -213,16 +224,16 @@ def tile_coarsepyramid_pa_kernel(
                     for c in range(2):
                         bp = 2 * i + c
                         nc.scalar.activation(
-                            out=tb[:, tau, c * 64:(c + 1) * 64], in_=y[:, u, c * 64:(c + 1) * 64], func=ACT.Relu,
+                            out=fs[:, c, tau, :], in_=y[:, u, c * 64:(c + 1) * 64], func=ACT.Relu,
                             bias=shift[:, tau, bp:bp + 1], scale=gain[:, tau, bp:bp + 1],
                         )
-            return tb
 
         def level(tb, k):
-            return tb[:, :, OFF[k]:OFF[k] + 2 * NV[k]].rearrange("p a (c t) -> p a c t", c=2)
+            return tb[:, :, OFF[k] - 128:OFF[k] - 128 + 2 * NV[k]].rearrange("p a (c t) -> p a c t", c=2)
 
         def front_b(i, tb, after_tables):
-            f = level(tb, 0)
+            fs = feats[i]
+            f = fs[:].rearrange("p c a t -> p a c t")
             m2 = m2p.tile([P, 8, 2, 63], F32, tag="m2")
             nc.vector.tensor_tensor(out=m2[:], in0=f[:, :, :, 0:63], in1=f[:, :, :, 1:64], op=ALU.max)
             nc.vector.tensor_tensor(out=level(tb, 1), in0=m2[:, :, :, 0:62], in1=m2[:, :, :, 1:63], op=ALU.max)
@@ -235,29 +246,39 @@ def tile_coarsepyramid_pa_kernel(
             if after_tables is not None:
                 after_tables()
             area = place(i)
-            for g in range(3):
-                nr = min(2, 5 - 2 * g)
+            tsb0 = tsp0.tile([P, 2, 512], F32, tag="tsb0")
+            for c in range(2):
+                tp = ps_tp.tile([P, 4, 128], F32, tag="tp")
+                for k in range(4):
+                    nc.tensor.transpose(
+                        tp[:, k, :], fs[:, c, 2 * k:2 * k + 2, :].rearrange("p a t -> p (a t)"), ident[:]
+                    )
+                nc.scalar.copy(out=tsb0[:, c, :], in_=tp[:].rearrange("p k q -> p (k q)"))
+            for c in range(2):
+                for v in range(2):
+                    nc.sync.dma_start(
+                        out=park0[area][v][64 * c:64 * c + 64],
+                        in_=tsb0[64 * v:64 * v + 64, c, :].rearrange("p (k q) -> p k q", k=4),
+                    )
+            for g in range(2):
                 tsb = tsp.tile([P, 2, 2, 512], F32, tag="tsb")
-                for rl in range(nr):
-                    r = 2 * g + rl
+                for rl in range(2):
+                    r = 1 + 2 * g + rl
                     for s in range(2):
                         tp = ps_tp.tile([P, 4, 128], F32, tag="tp")
                         for u in range(4):
-                            nc.tensor.transpose(tp[:, u, :], tb[:, 4 * s + u, r * 128:(r + 1) * 128], ident[:])
+                            nc.tensor.transpose(tp[:, u, :], tb[:, 4 * s + u, (r - 1) * 128:r * 128], ident[:])
                         nc.scalar.copy(out=tsb[:, rl, s, :], in_=tp[:].rearrange("p u q -> p (u q)"))
-                nump = P if (g < 2 or i < 4) else ZERO0 - 512
-                nc.sync.dma_start(
-                    out=parkv[area][0:nump, 2 * g:2 * g + nr, :],
-                    in_=tsb[0:nump, 0:nr, :, :].rearrange("p r s e -> p r (s e)"),
-                )
+                if g == 0 or i < 4:
+                    nc.sync.dma_start(
+                        out=parkv[area][:, 1 + 2 * g:3 + 2 * g, :], in_=tsb[:].rearrange("p r s e -> p r (s e)")
+                    )
+                else:
+                    for rl, nump in ((0, P), (1, ZERO0 - 512)):
+                        nc.sync.dma_start(
+                            out=parkv[area][0:nump, 3 + rl, :], in_=tsb[0:nump, rl, :, :].rearrange("p s e -> p (s e)")
+                        )
             late = i >= NPAIR - NHOLD
-            if late:
-                fs = pools["hold"].tile([P, 2, 8, 64], F32, name="fsh%d" % i)
-                held0.append((i, fs))
-            else:
-                fs = fsp.tile([P, 2, 8, 64], F32, tag="fs")
-            for c in range(2):
-                nc.scalar.copy(out=fs[:, c, :, :], in_=tb[:, :, c * 64:(c + 1) * 64])
             if not late:
                 store_out0(i, fs)
             got = []
@@ -388,6 +409,20 @@ def tile_coarsepyramid_pa_kernel(
                 nc.scalar.activation(out=warm[:, 1:2], in_=warm[:, 0:1], func=ACT.Sqrt)
                 nc.vector.tensor_copy(out=pv[:].rearrange("p m s u o -> p m (s u o)"), in_=pv_bf[:, :, 0:8])
 
+                widened = {}
+                for k in range(S_CHUNKS):
+                    q0, q1 = FEAT_CHUNKS[k]
+                    planes = prep2.tile([P, 4, (q1 - q0) * 64], BF16, tag="planes")
+                    for j in range(4):
+                        nc.scalar.activation(
+                            out=planes[:, j, :],
+                            in_=xb[:, j, q0:q1, :].rearrange("p b t -> p (b t)").bitcast(FP8),
+                            func=ACT.Copy, scale=sc[:, j:j + 1],
+                        )
+                    gxs = prep.tile([P, (q1 - q0) * 64, 4], BF16, name="gxs%d" % k, align_bytes=64)
+                    nc.scalar.copy(out=gxs[:], in_=planes[:].rearrange("p j c -> p c j"))
+                    widened[q0] = gxs
+
                 def row_indices():
                     xs = prep.tile([P, 96], F32)
                     nc.vector.tensor_scalar(
@@ -487,12 +522,24 @@ def tile_coarsepyramid_pa_kernel(
 
                 def feat_chunk(p0, p1):
                     n = p1 - p0
-                    gx = prep2.tile([P, n * 64, 4], BF16, tag="gx", align_bytes=64)
-                    for j in range(4):
-                        nc.vector.tensor_scalar(
-                            out=gx[:, :, j], in0=xb[:, j, p0:p1, :].rearrange("p b t -> p (b t)").bitcast(FP8),
-                            scalar1=sc[:, j:j + 1], scalar2=None, op0=ALU.mult,
-                        )
+                    if p0 in widened:
+                        gx = widened[p0]
+                    elif p0 < S_BATCHES:
+                        pl = prep2.tile([P, 4, n * 64], BF16, tag="planes")
+                        for j in range(4):
+                            nc.scalar.activation(
+                                out=pl[:, j, :], in_=xb[:, j, p0:p1, :].rearrange("p b t -> p (b t)").bitcast(FP8),
+                                func=ACT.Copy, scale=sc[:, j:j + 1],
+                            )
+                        gx = prep2.tile([P, n * 64, 4], BF16, tag="gx", align_bytes=64)
+                        nc.scalar.copy(out=gx[:], in_=pl[:].rearrange("p j c -> p c j"))
+                    else:
+                        gx = prep2.tile([P, n * 64, 4], BF16, tag="gx", align_bytes=64)
+                        for j in range(4):
+                            nc.vector.tensor_scalar(
+                                out=gx[:, :, j], in0=xb[:, j, p0:p1, :].rearrange("p b t -> p (b t)").bitcast(FP8),
+                                scalar1=sc[:, j:j + 1], scalar2=None, op0=ALU.mult,
+                            )
                     nc.vector.quantize_mx(
                         out=xcodes[:, p0 * 64:p1 * 64].bitcast(FP8X4),
                         scales=xscales[:, p0 * 64:p1 * 64],

@@ -231,7 +231,8 @@ def tile_coarsepyramid_pa_kernel(
         def level(tb, k):
             return tb[:, :, OFF[k] - 128:OFF[k] - 128 + 2 * NV[k]].rearrange("p a (c t) -> p a c t", c=2)
 
-        def front_b(i, tb, after_tables):
+        def tables(i):
+            tb = tbs[i % NTB]
             fs = feats[i]
             f = fs[:].rearrange("p c a t -> p a c t")
             m2 = m2p.tile([P, 8, 2, 63], F32, tag="m2")
@@ -243,8 +244,10 @@ def tile_coarsepyramid_pa_kernel(
                     out=level(tb, k), in0=prev[:, :, :, 0:NV[k]], in1=prev[:, :, :, WID[k - 1]:WID[k - 1] + NV[k]],
                     op=ALU.max,
                 )
-            if after_tables is not None:
-                after_tables()
+
+        def rows_out(i):
+            tb = tbs[i % NTB]
+            fs = feats[i]
             area = place(i)
             tsb0 = tsp0.tile([P, 2, 512], F32, tag="tsb0")
             for c in range(2):
@@ -366,18 +369,21 @@ def tile_coarsepyramid_pa_kernel(
             ahead = min(NPAIR, j + 5)
             if j == 0:
                 activations(0, feat_chunk)
-                front_b(0, tbs[0], after_tables)
+                tables(0)
+                rows_out(0)
                 activations(1, feat_chunk)
             else:
                 if j + 1 < NPAIR:
                     activations(j + 1, feat_chunk)
                 if done[0] < ahead:
                     stats_one(feat_chunk)
+                if j - 1 >= LAG:
+                    back(j - 1 - LAG)
                 if j < NPAIR:
-                    front_b(j, tbs[j % NTB], after_tables)
-            if j >= LAG:
-                back(j - LAG)
-            late_stores(j)
+                    tables(j)
+                if 2 <= j <= NPAIR:
+                    rows_out(j - 1)
+            late_stores(j - 1)
             while done[0] < ahead:
                 stats_one(feat_chunk)
             features_for(min(NPAIR, j + 8), feat_chunk)
@@ -571,5 +577,5 @@ def tile_coarsepyramid_pa_kernel(
                 step(j, feat_chunk, None)
 
         pools["hold"] = ctx.enter_context(tc.tile_pool(name="hold", bufs=1))
-        for j in range(SPLIT_STEP, NPAIR + LAG):
+        for j in range(SPLIT_STEP, NPAIR + LAG + 1):
             step(j, None, None)

from contextlib import ExitStack

import concourse.bass as bass
import concourse.mybir as mybir
from concourse.masks import make_block_diagonal, make_identity

F32 = mybir.dt.float32
BF16 = mybir.dt.bfloat16
I32 = mybir.dt.int32
U32 = mybir.dt.uint32
U8 = mybir.dt.uint8
FP8 = mybir.dt.float8_e4m3fn
FP8X4 = mybir.dt.float8_e4m3fn_x4
ALU = mybir.AluOpType
ACT = mybir.ActivationFunctionType
AX = mybir.AxisListType

FLOPS = 2 * 48 * 1024 * 512 * 64

P = 128
NB = 48
NPAIR = 24
NFOUR = 14
NHOLD = 5
PARK_ROWS = 1280
WID = (1, 3, 6, 12, 24, 48)
NV = (64, 62, 59, 53, 41, 17)
OFF = (0, 128, 252, 370, 476, 558)
NENT = 640
ZERO0 = 592
EPS = 1e-5
LAG = 3
NTB = 2
STAT_GROUPS = ((0, 1), (1, 3), (3, 6), (6, 9), (9, 12), (12, 15), (15, 18), (18, 21), (21, 24))
BYTE_LOADS = ((0, 4), (4, 16), (16, 28), (28, 38), (38, 48))
FEAT_CHUNKS = ((0, 2), (2, 4), (4, 8), (8, 12), (12, 16), (16, 20), (20, 24), (24, 28), (28, 32), (32, 36), (36, 40), (40, 44), (44, 48))
HEAD_STEPS = 2
S_CHUNKS = 4
S_BATCHES = 32
SPLIT_STEP = 18


def tile_coarsepyramid_pa_kernel(
    tc, feature_bytes, feature_scale, segments, w_lr, b_lr, g_lr, be_lr, out_0, out_1
):
    nc = tc.nc
    with ExitStack() as ctx:
        const = ctx.enter_context(tc.tile_pool(name="const", bufs=1))
        small = ctx.enter_context(tc.tile_pool(name="small", bufs=2))
        ps_y = ctx.enter_context(tc.psum_pool(name="ps_y", bufs=2))
        ps_tp = ctx.enter_context(tc.psum_pool(name="ps_tp", bufs=3))
        ps_bk = ctx.enter_context(tc.psum_pool(name="ps_bk", bufs=2))
        ps_st = ctx.enter_context(tc.psum_pool(name="ps_st", bufs=1))
        tabs = ctx.enter_context(tc.tile_pool(name="tabs", bufs=1))
        fsp = ctx.enter_context(tc.tile_pool(name="fsp", bufs=5))
        m2p = ctx.enter_context(tc.tile_pool(name="m2p", bufs=1))
        tsp = ctx.enter_context(tc.tile_pool(name="tsp", bufs=4))
        tsp0 = ctx.enter_context(tc.tile_pool(name="tsp0", bufs=3))
        gp = ctx.enter_context(tc.tile_pool(name="gp", bufs=2 * (LAG + 1)))
        o1p = ctx.enter_context(tc.tile_pool(name="o1p", bufs=4))
        etp = ctx.enter_context(tc.tile_pool(name="etp", bufs=2))

        ident = const.tile([P, P], F32)
        make_identity(nc, ident[:])
        ones8 = const.tile([P, P], F32)
        make_block_diagonal(nc, ones8[:], 8)

        xcodes = const.tile([P, NB * 64], U32, align_bytes=64)
        xscales = const.tile([P, NB * 64], U8, align_bytes=64)
        wcodes = const.tile([P, 1024], U32, align_bytes=64)
        wscales = const.tile([P, 1024], U8, align_bytes=64)
        stats = const.tile([P, 8, NB, 3], F32)
        gain = const.tile([P, 8, NB], F32)
        shift = const.tile([P, 8, NB], F32)
        idx = const.tile([P, 2, 48], I32)
        pv = const.tile([P, 3, 2, 4, 1], F32)
        sc = const.tile([P, 4], F32)
        warm = const.tile([P, 2], F32)
        nc.gpsimd.memset(warm[:], 1.0)
        side_i = const.tile([P, 48], I32)
        nc.gpsimd.iota(side_i[:], pattern=[[0, 24], [1, 2]], base=0, channel_multiplier=0)
        pidx = const.tile([P, 1], I32)
        nc.gpsimd.iota(pidx[:], pattern=[[0, 1]], base=0, channel_multiplier=1)

        tbs = []
        for r in range(NTB):
            tb = tabs.tile([P, 8, NENT - 128], F32, name="tb%d" % r)
            nc.gpsimd.memset(tb[:, :, ZERO0 - 128:NENT - 128], 0.0)
            tbs.append(tb)

        flat = [o.rearrange("b (x y) n -> (b x) (y n)", y=8) for o in (out_1, out_0)]
        rows = [flat[k % 2][0:(1 + k // 2) * PARK_ROWS, :] for k in range(4)]
        spots = [flat[k % 2][(k // 2) * PARK_ROWS:(1 + k // 2) * PARK_ROWS, :] for k in range(4)]

        def which(i):
            if i < NFOUR:
                return i + 10
            return i - 9 if i < NPAIR - NHOLD else i - (NPAIR - NHOLD)

        def place(i):
            return i % 4 if i < NFOUR else i % 2

        parkv = [r.rearrange("(p r s) e -> p r (s e)", p=P, s=2) for r in spots]
        park0 = [pk[:, 0, :].rearrange("p (k v q) -> v p k q", k=4, v=2) for pk in parkv]
        o0v = out_0.rearrange("b (s q u) t -> q (b s) (u t)", s=2, u=4)
        o1v = out_1.rearrange("b (s q u) n -> q (b s) (u n)", s=2, u=4)

        def conv(i, s):
            y = ps_y.tile([P, 4, 128], F32, tag="y")
            for u in range(4):
                tau = 4 * s + u
                nc.tensor.matmul_mx(
                    out=y[:, u, :],
                    lhsT=wcodes[:, tau * 128:(tau + 1) * 128].bitcast(FP8X4),
                    lhsT_scale=wscales[:, tau * 128:(tau + 1) * 128],
                    rhs=xcodes[:, i * 128:(i + 1) * 128].bitcast(FP8X4),
                    rhs_scale=xscales[:, i * 128:(i + 1) * 128],
                    start=True,
                    stop=True,
                )
            return y

        def pair_stats(i):
            for s in range(2):
                y = conv(i, s)
                for u in range(4):
                    nc.vector.bn_stats(
                        out=stats[:, 4 * s + u, 2 * i:2 * i + 2, :].rearrange("p c f -> p (c f)"),
                        in_=y[:, u, :].rearrange("p (c t) -> p t c", c=2),
                    )

        def group_affine(p0, p1):
            b0, b1 = 2 * p0, 2 * p1
            nb = b1 - b0
            bias_c = pv[:, 0, :, :, :]
            g_c = pv[:, 1, :, :, :]
            be_c = pv[:, 2, :, :, :]
            mp = small.tile([P, 8, nb], F32, tag="mp")
            nc.vector.tensor_tensor(
                out=mp[:], in0=stats[:, :, b0:b1, 1],
                in1=bias_c.rearrange("p s u o -> p (s u) o").to_broadcast([P, 8, nb]), op=ALU.add,
            )
            sq = small.tile([P, 8, nb], F32, tag="sq")
            nc.vector.tensor_tensor(out=sq[:], in0=mp[:], in1=mp[:], op=ALU.mult)
            v2 = small.tile([P, 8, nb], F32, tag="v2")
            nc.vector.scalar_tensor_tensor(
                out=v2[:], in0=stats[:, :, b0:b1, 2], scalar=1.0 / 64.0, in1=sq[:],
                op0=ALU.mult, op1=ALU.add,
            )
            rs = small.tile([P, 2, 2, nb], F32, tag="rs")
            for s in range(2):
                for a, src in enumerate((mp, v2)):
                    nc.vector.tensor_reduce(
                        out=rs[:, a, s, :],
                        in_=src[:, 4 * s:4 * s + 4, :].rearrange("p u b -> p b u"),
                        axis=AX.X, op=ALU.add,
                    )
            pst = ps_st.tile([P, 4 * nb], F32, tag="pst")
            nc.tensor.matmul(
                out=pst[:], lhsT=ones8[:], rhs=rs[:].rearrange("p a s b -> p (a s b)"), start=True, stop=True
            )
            mu = small.tile([P, 2, 1, nb], F32, tag="mu")
            muf = mu[:].rearrange("p s o b -> p (s o b)")
            nc.vector.tensor_scalar(out=muf, in0=pst[:, 0:2 * nb], scalar1=1.0 / 32.0, scalar2=None, op0=ALU.mult)
            msq = small.tile([P, 2 * nb], F32, tag="msq")
            nc.vector.tensor_tensor(out=msq[:], in0=muf, in1=muf, op=ALU.mult)
            var = small.tile([P, 2 * nb], F32, tag="var")
            nc.vector.scalar_tensor_tensor(
                out=var[:], in0=pst[:, 2 * nb:4 * nb], scalar=1.0 / 32.0, in1=msq[:], op0=ALU.mult, op1=ALU.subtract
            )
            sd = small.tile([P, 2 * nb], F32, tag="sd")
            nc.scalar.activation(out=sd[:], in_=var[:], func=ACT.Sqrt, bias=EPS)
            rstd = small.tile([P, 2, 1, nb], F32, tag="rstd")
            nc.vector.reciprocal(out=rstd[:].rearrange("p s o b -> p (s o b)"), in_=sd[:])
            full = [P, 2, 4, nb]
            gn = gain[:, :, b0:b1].rearrange("p (s u) b -> p s u b", s=2)
            sh = shift[:, :, b0:b1].rearrange("p (s u) b -> p s u b", s=2)
            nc.vector.tensor_tensor(out=gn, in0=rstd[:].to_broadcast(full), in1=g_c.to_broadcast(full), op=ALU.mult)
            t1 = small.tile([P, 2, 4, nb], F32, tag="t1")
            nc.vector.tensor_tensor(
                out=t1[:], in0=bias_c.to_broadcast(full), in1=mu[:].to_broadcast(full), op=ALU.subtract
            )
            nc.vector.tensor_tensor(out=t1[:], in0=t1[:], in1=gn, op=ALU.mult)
            nc.vector.tensor_tensor(out=sh, in0=t1[:], in1=be_c.to_broadcast(full), op=ALU.add)

        def store_out0(i, fs):
            b0 = 2 * which(i)
            nc.sync.dma_start(
                out=o0v[:, 2 * b0:2 * b0 + 4, :], in_=fs[:].rearrange("q c (s u) t -> q (c s) (u t)", s=2)
            )

        def store_out1(i, o1):
            b0 = 2 * which(i)
            nc.sync.dma_start(out=o1v[:, 2 * b0:2 * b0 + 4, :], in_=o1[:].rearrange("q c s u n -> q (c s) (u n)"))

        pending = [[], []]

        def flush(area):
            for i, t in pending[area]:
                if area == 0:
                    store_out1(i, t)
                else:
                    store_out0(i, t)
            pending[area].clear()

        held0 = []
        held1 = []
        gathered = {}
        pools = {}

        feats = {}

        def front_a(i):
            if i >= NPAIR - NHOLD:
                fs = pools["hold"].tile([P, 2, 8, 64], F32, name="fsh%d" % i)
                held0.append((i, fs))
            else:
                fs = fsp.tile([P, 2, 8, 64], F32, tag="fs")
            feats[i] = fs
            for s in range(2):
                y = conv(i, s)
                for u in range(4):
                    tau = 4 * s + u
                    for c in range(2):
                        bp = 2 * i + c
                        nc.scalar.activation(
                            out=fs[:, c, tau, :], in_=y[:, u, c * 64:(c + 1) * 64], func=ACT.Relu,
                            bias=shift[:, tau, bp:bp + 1], scale=gain[:, tau, bp:bp + 1],
                        )

        def level(tb, k):
            return tb[:, :, OFF[k] - 128:OFF[k] - 128 + 2 * NV[k]].rearrange("p a (c t) -> p a c t", c=2)

        def tables(i):
            tb = tbs[i % NTB]
            fs = feats[i]
            f = fs[:].rearrange("p c a t -> p a c t")
            m2 = m2p.tile([P, 8, 2, 63], F32, tag="m2")
            nc.vector.tensor_tensor(out=m2[:], in0=f[:, :, :, 0:63], in1=f[:, :, :, 1:64], op=ALU.max)
            nc.vector.tensor_tensor(out=level(tb, 1), in0=m2[:, :, :, 0:62], in1=m2[:, :, :, 1:63], op=ALU.max)
            for k in range(2, 6):
                prev = level(tb, k - 1)
                nc.vector.tensor_tensor(
                    out=level(tb, k), in0=prev[:, :, :, 0:NV[k]], in1=prev[:, :, :, WID[k - 1]:WID[k - 1] + NV[k]],
                    op=ALU.max,
                )

        def rows_out(i):
            tb = tbs[i % NTB]
            fs = feats[i]
            area = place(i)
            tsb0 = tsp0.tile([P, 2, 512], F32, tag="tsb0")
            for c in range(2):
                tp = ps_tp.tile([P, 4, 128], F32, tag="tp")
                for k in range(4):
                    nc.tensor.transpose(
                        tp[:, k, :], fs[:, c, 2 * k:2 * k + 2, :].rearrange("p a t -> p (a t)"), ident[:]
                    )
                nc.scalar.copy(out=tsb0[:, c, :], in_=tp[:].rearrange("p k q -> p (k q)"))
            for c in range(2):
                for v in range(2):
                    nc.sync.dma_start(
                        out=park0[area][v][64 * c:64 * c + 64],
                        in_=tsb0[64 * v:64 * v + 64, c, :].rearrange("p (k q) -> p k q", k=4),
                    )
            for g in range(2):
                tsb = tsp.tile([P, 2, 2, 512], F32, tag="tsb")
                for rl in range(2):
                    r = 1 + 2 * g + rl
                    for s in range(2):
                        tp = ps_tp.tile([P, 4, 128], F32, tag="tp")
                        for u in range(4):
                            nc.tensor.transpose(tp[:, u, :], tb[:, 4 * s + u, (r - 1) * 128:r * 128], ident[:])
                        nc.scalar.copy(out=tsb[:, rl, s, :], in_=tp[:].rearrange("p u q -> p (u q)"))
                if g == 0 or i < 4:
                    nc.sync.dma_start(
                        out=parkv[area][:, 1 + 2 * g:3 + 2 * g, :], in_=tsb[:].rearrange("p r s e -> p r (s e)")
                    )
                else:
                    for rl, nump in ((0, P), (1, ZERO0 - 512)):
                        nc.sync.dma_start(
                            out=parkv[area][0:nump, 3 + rl, :], in_=tsb[0:nump, rl, :, :].rearrange("p s e -> p (s e)")
                        )
            late = i >= NPAIR - NHOLD
            if not late:
                store_out0(i, fs)
            got = []
            for s in range(2):
                col = 2 * which(i) + s
                pairg = []
                for e in range(2):
                    g = gp.tile([P, 512], F32, tag="g%d" % e)
                    nc.gpsimd.indirect_dma_start(
                        out=g[:], out_offset=None, in_=rows[area],
                        in_offset=bass.IndirectOffsetOnAxis(ap=idx[:, e, col:col + 1], axis=0),
                    )
                    pairg.append(g)
                got.append(pairg)
            gathered[i] = got
        def back(i):
            late = i >= NPAIR - NHOLD
            if late:
                o1 = pools["hold"].tile([P, 2, 2, 4, 64], F32, name="o1h%d" % i)
                held1.append((i, o1))
            else:
                o1 = o1p.tile([P, 2, 2, 4, 64], F32, tag="o1")
            for s in range(2):
                ga, ge = gathered[i][s]
                if s == 1:
                    bkb = ps_bk.tile([P, 4, 128], F32, tag="bk")
                    for u in range(4):
                        nc.tensor.transpose(bkb[:, u, :], ge[:, u * 128:(u + 1) * 128], ident[:])
                    bka = ps_bk.tile([P, 4, 128], F32, tag="bk")
                    for u in range(4):
                        nc.tensor.transpose(bka[:, u, :], ga[:, u * 128:(u + 1) * 128], ident[:])
                    et = etp.tile([P, 4, 128], F32, tag="et")
                    nc.scalar.copy(out=et[:], in_=bkb[:])
                    nc.vector.tensor_tensor(
                        out=o1[:, :, s, :, :], in0=bka[:].rearrange("q u (c n) -> q c u n", c=2),
                        in1=et[:].rearrange("q u (c n) -> q c u n", c=2), op=ALU.max,
                    )
                for h in range(2 - 2 * s):
                    bk = ps_bk.tile([P, 2, 2, 128], F32, tag="bk")
                    for ul in range(2):
                        u = 2 * h + ul
                        for e, g in enumerate((ga, ge)):
                            nc.tensor.transpose(bk[:, e, ul, :], g[:, u * 128:(u + 1) * 128], ident[:])
                    nc.vector.tensor_reduce(
                        out=o1[:, :, s, 2 * h:2 * h + 2, :].rearrange("q c u n -> q u c n"),
                        in_=bk[:].rearrange("q e u (c n) -> q u c n e", c=2),
                        axis=AX.X, op=ALU.max,
                    )
            if not late:
                store_out1(i, o1)

        done = [0, 0, 0]

        def features_for(npairs, feat_chunk):
            while done[2] < len(FEAT_CHUNKS) and FEAT_CHUNKS[done[2]][0] < 2 * npairs:
                feat_chunk(FEAT_CHUNKS[done[2]][0], FEAT_CHUNKS[done[2]][1])
                done[2] += 1

        def stats_one(feat_chunk):
            features_for(done[0] + 1, feat_chunk)
            pair_stats(done[0])
            done[0] += 1
            if done[0] == STAT_GROUPS[done[1]][1]:
                group_affine(STAT_GROUPS[done[1]][0], STAT_GROUPS[done[1]][1])
                done[1] += 1

        def late_stores(j):
            if j >= NPAIR - 2:
                flush(0)
                for i, o1 in held1:
                    store_out1(i, o1)
                held1.clear()
            if j >= NPAIR - 1:
                flush(1)
                for i, f0 in held0:
                    store_out0(i, f0)
                held0.clear()

        def activations(i, feat_chunk):
            while done[1] < len(STAT_GROUPS) and STAT_GROUPS[done[1]][0] <= i:
                stats_one(feat_chunk)
            front_a(i)

        def step(j, feat_chunk, after_tables):
            ahead = min(NPAIR, j + 5)
            if j == 0:
                activations(0, feat_chunk)
                tables(0)
                rows_out(0)
                activations(1, feat_chunk)
            else:
                if j + 1 < NPAIR:
                    activations(j + 1, feat_chunk)
                if done[0] < ahead:
                    stats_one(feat_chunk)
                if j - 1 >= LAG:
                    back(j - 1 - LAG)
                if j < NPAIR:
                    tables(j)
                if 2 <= j <= NPAIR:
                    rows_out(j - 1)
            late_stores(j - 1)
            while done[0] < ahead:
                stats_one(feat_chunk)
            features_for(min(NPAIR, j + 8), feat_chunk)

        with tc.tile_pool(name="prep", bufs=1) as prep, tc.tile_pool(name="prep2", bufs=2) as prep2:
            with tc.manual_schedule():
                xb = prep.tile([P, 4, NB, 64], U8)
                fv = feature_bytes.rearrange("b (p j) t -> j p b t", j=4)
                w_sb = prep.tile([P, 2, 4, 512], BF16)
                nc.sync.dma_start(out=sc[:], in_=feature_scale.rearrange("o (p j) i -> p (o j i)", j=4))
                sg_bf = prep.tile([P, NPAIR, 4], BF16)
                seg_v = segments.rearrange("(i c) n f -> c n i f", c=2)
                for c in range(2):
                    nc.sync.dma_start(out=sg_bf[c * 64:(c + 1) * 64, :, :], in_=seg_v[c])
                pv_bf = prep.tile([P, 3, 16], BF16)
                for m, vec in enumerate((b_lr, g_lr, be_lr)):
                    nc.sync.dma_start(
                        out=pv_bf[:, m, 0:8].rearrange("q (s u) -> q s u", s=2),
                        in_=vec.rearrange("(s q u) -> q s u", s=2, u=4),
                    )
                nc.sync.dma_start(
                    out=w_sb[:].rearrange("q s u k -> q s (u k)"),
                    in_=w_lr.rearrange("(s q u) k -> q s (u k)", s=2, u=4),
                )
                for p0, p1 in BYTE_LOADS:
                    b0 = 2 * which(p0 // 2)
                    for j in range(4):
                        nc.sync.dma_start(out=xb[:, j, p0:p1, :], in_=fv[j][:, b0:b0 + (p1 - p0), :])
                nc.scalar.activation(out=warm[:, 1:2], in_=warm[:, 0:1], func=ACT.Sqrt)
                nc.vector.tensor_copy(out=pv[:].rearrange("p m s u o -> p m (s u o)"), in_=pv_bf[:, :, 0:8])

                widened = {}
                for k in range(S_CHUNKS):
                    q0, q1 = FEAT_CHUNKS[k]
                    planes = prep2.tile([P, 4, (q1 - q0) * 64], BF16, tag="planes")
                    for j in range(4):
                        nc.scalar.activation(
                            out=planes[:, j, :],
                            in_=xb[:, j, q0:q1, :].rearrange("p b t -> p (b t)").bitcast(FP8),
                            func=ACT.Copy, scale=sc[:, j:j + 1],
                        )
                    gxs = prep.tile([P, (q1 - q0) * 64, 4], BF16, name="gxs%d" % k, align_bytes=64)
                    nc.scalar.copy(out=gxs[:], in_=planes[:].rearrange("p j c -> p c j"))
                    widened[q0] = gxs

                def row_indices():
                    xs = prep.tile([P, 96], F32)
                    nc.vector.tensor_scalar(
                        out=xs[:], in0=sg_bf[:].rearrange("p i f -> p (i f)"), scalar1=0.0, scalar2=63.0,
                        op0=ALU.max, op1=ALU.min,
                    )
                    xi = prep.tile([P, 96], I32)
                    nc.vector.tensor_copy(out=xi[:], in_=xs[:])
                    xf = prep.tile([P, 96], F32)
                    nc.vector.tensor_copy(out=xf[:], in_=xi[:])
                    gt = prep.tile([P, 96], F32)
                    nc.vector.tensor_tensor(out=gt[:], in0=xf[:], in1=xs[:], op=ALU.is_gt)
                    fl = prep.tile([P, 48, 2], F32)
                    nc.vector.tensor_tensor(
                        out=fl[:].rearrange("p c e -> p (c e)"), in0=xf[:], in1=gt[:], op=ALU.subtract
                    )
                    lo = fl[:, :, 0]
                    hi = fl[:, :, 1]
                    lm = prep.tile([P, 48], F32)
                    nc.vector.tensor_tensor(out=lm[:], in0=hi, in1=lo, op=ALU.subtract)
                    fa = prep.tile([P, 48, 5], F32)
                    fd = prep.tile([P, 48, 5], F32)
                    for j in range(1, 6):
                        thr = float(WID[j] - 1)
                        nc.vector.tensor_scalar(
                            out=fa[:, :, j - 1], in0=lm[:], scalar1=thr, scalar2=float(4 * NV[j - 1]),
                            op0=ALU.is_ge, op1=ALU.mult,
                        )
                        nc.vector.tensor_scalar(
                            out=fd[:, :, j - 1], in0=lm[:], scalar1=thr, scalar2=float(2 * (WID[j] - WID[j - 1])),
                            op0=ALU.is_ge, op1=ALU.mult,
                        )
                    sa = prep.tile([P, 48], F32)
                    nc.vector.tensor_reduce(out=sa[:], in_=fa[:], axis=AX.X, op=ALU.add)
                    sd2 = prep.tile([P, 48], F32)
                    nc.vector.tensor_reduce(out=sd2[:], in_=fd[:], axis=AX.X, op=ALU.add)
                    side = prep.tile([P, 48], F32)
                    nc.vector.tensor_copy(out=side[:], in_=side_i[:])
                    pint = prep.tile([P, 2], I32)
                    nc.vector.tensor_single_scalar(out=pint[:, 0:1], in_=pidx[:], scalar=6, op=ALU.logical_shift_right)
                    nc.vector.tensor_single_scalar(out=pint[:, 1:2], in_=pidx[:], scalar=31, op=ALU.bitwise_and)
                    pfl = prep.tile([P, 2], F32)
                    nc.vector.tensor_copy(out=pfl[:], in_=pint[:])
                    c128 = prep.tile([P, 1], F32)
                    nc.vector.tensor_scalar(out=c128[:], in0=pfl[:, 0:1], scalar1=128.0, scalar2=None, op0=ALU.mult)
                    zc = prep.tile([P, 1], F32)
                    nc.vector.tensor_scalar(
                        out=zc[:], in0=pfl[:, 1:2], scalar1=2.0, scalar2=float(2 * ZERO0), op0=ALU.mult, op1=ALU.add
                    )
                    zidx = prep.tile([P, 48], F32)
                    nc.vector.tensor_scalar(out=zidx[:], in0=side[:], scalar1=zc[:, 0:1], scalar2=None, op0=ALU.add)
                    cd = prep.tile([P, 48], F32)
                    nc.vector.tensor_scalar(out=cd[:], in0=sd2[:], scalar1=pfl[:, 0:1], scalar2=None, op0=ALU.mult)
                    com = prep.tile([P, 48], F32)
                    nc.vector.tensor_tensor(out=com[:], in0=sa[:], in1=cd[:], op=ALU.subtract)
                    nc.vector.tensor_tensor(out=com[:], in0=com[:], in1=side[:], op=ALU.add)
                    nc.vector.tensor_scalar(out=com[:], in0=com[:], scalar1=c128[:, 0:1], scalar2=None, op0=ALU.add)
                    for e, (pos, thr) in enumerate(((lo, 0.0), (hi, 1.0))):
                        ri = prep.tile([P, 48], F32, name="ri%d" % e)
                        nc.vector.scalar_tensor_tensor(
                            out=ri[:], in0=pos, scalar=2.0, in1=com[:], op0=ALU.mult, op1=ALU.add
                        )
                        if e == 1:
                            nc.vector.tensor_tensor(out=ri[:], in0=ri[:], in1=sd2[:], op=ALU.subtract)
                        nc.vector.tensor_tensor(out=ri[:], in0=ri[:], in1=zidx[:], op=ALU.subtract)
                        ne = prep.tile([P, 48], F32, name="ne%d" % e)
                        nc.vector.tensor_single_scalar(out=ne[:], in_=lm[:], scalar=thr, op=ALU.is_ge)
                        nc.vector.tensor_tensor(out=ri[:], in0=ri[:], in1=ne[:], op=ALU.mult)
                        nc.vector.tensor_tensor(out=ri[:], in0=ri[:], in1=zidx[:], op=ALU.add)
                        nc.vector.tensor_copy(out=idx[:, e, :], in_=ri[:])
                    part = prep.tile([P, 3, 96], I32)
                    idf = idx[:].rearrange("p e c -> p (e c)")
                    nc.vector.tensor_single_scalar(out=part[:, 0, :], in_=idf, scalar=8, op=ALU.logical_shift_right)
                    nc.vector.tensor_scalar(
                        out=part[:, 1, :], in0=idf, scalar1=1, scalar2=127,
                        op0=ALU.logical_shift_right, op1=ALU.bitwise_and,
                    )
                    nc.vector.tensor_single_scalar(out=part[:, 2, :], in_=idf, scalar=1, op=ALU.bitwise_and)
                    partf = prep.tile([P, 3, 96], F32)
                    nc.vector.tensor_copy(out=partf[:], in_=part[:])
                    nc.vector.scalar_tensor_tensor(
                        out=partf[:, 2, :], in0=partf[:, 1, :], scalar=10.0, in1=partf[:, 2, :], op0=ALU.mult, op1=ALU.add
                    )
                    nc.vector.scalar_tensor_tensor(
                        out=partf[:, 2, :], in0=partf[:, 0, :], scalar=2.0, in1=partf[:, 2, :], op0=ALU.mult, op1=ALU.add
                    )
                    for i in range(NFOUR):
                        if place(i) >= 2 and place(i) % 2 == 0:
                            c0 = 2 * which(i)
                            upper = partf[:, 2, :].rearrange("p (e c) -> p e c", e=2)[:, :, c0:c0 + 4]
                            nc.vector.tensor_scalar(
                                out=upper, in0=upper, scalar1=float(PARK_ROWS), scalar2=None, op0=ALU.add
                            )
                    nc.vector.tensor_copy(out=idf, in_=partf[:, 2, :])

                row_indices()

                def feat_chunk(p0, p1):
                    n = p1 - p0
                    if p0 in widened:
                        gx = widened[p0]
                    elif p0 < S_BATCHES:
                        pl = prep2.tile([P, 4, n * 64], BF16, tag="planes")
                        for j in range(4):
                            nc.scalar.activation(
                                out=pl[:, j, :], in_=xb[:, j, p0:p1, :].rearrange("p b t -> p (b t)").bitcast(FP8),
                                func=ACT.Copy, scale=sc[:, j:j + 1],
                            )
                        gx = prep2.tile([P, n * 64, 4], BF16, tag="gx", align_bytes=64)
                        nc.scalar.copy(out=gx[:], in_=pl[:].rearrange("p j c -> p c j"))
                    else:
                        gx = prep2.tile([P, n * 64, 4], BF16, tag="gx", align_bytes=64)
                        for j in range(4):
                            nc.vector.tensor_scalar(
                                out=gx[:, :, j], in0=xb[:, j, p0:p1, :].rearrange("p b t -> p (b t)").bitcast(FP8),
                                scalar1=sc[:, j:j + 1], scalar2=None, op0=ALU.mult,
                            )
                    nc.vector.quantize_mx(
                        out=xcodes[:, p0 * 64:p1 * 64].bitcast(FP8X4),
                        scales=xscales[:, p0 * 64:p1 * 64],
                        in_=gx[:].rearrange("p c j -> p (c j)"),
                    )

                features_for(2, feat_chunk)

                wg = prep.tile([P, 8, 128, 4], BF16, align_bytes=64)
                for h in range(4):
                    xt = ps_tp.tile([P, 2, 2, 128], F32, tag="tp")
                    for a in range(2):
                        tau = 2 * h + a
                        words = w_sb[:, tau // 4, tau % 4, :].bitcast(F32)
                        for v in range(2):
                            nc.tensor.transpose(xt[:, a, v, :], words[:, v:256:2], ident[:])
                    nc.vector.tensor_copy(
                        out=wg[:, 2 * h:2 * h + 2, :, :].rearrange("p a q e -> p a (q e)").bitcast(F32)
                        .rearrange("p a (q v) -> p a q v", v=2),
                        in_=xt[:].rearrange("p a v q -> p a q v"),
                    )
                nc.vector.quantize_mx(
                    out=wcodes[:].bitcast(FP8X4), scales=wscales[:], in_=wg[:].rearrange("p a q e -> p (a q e)")
                )

                for j in range(HEAD_STEPS):
                    step(j, feat_chunk, None)
            for j in range(HEAD_STEPS, SPLIT_STEP):
                step(j, feat_chunk, None)

        pools["hold"] = ctx.enter_context(tc.tile_pool(name="hold", bufs=1))
        for j in range(SPLIT_STEP, NPAIR + LAG + 1):
            step(j, None, None)
